import numpy as np
import ml_dtypes


def mxq(x, axis, fmt="e4m3"):
    dtype, down = {"e4m3": (ml_dtypes.float8_e4m3fn, 7), "e5m2": (ml_dtypes.float8_e5m2, 14)}[fmt]
    v = np.moveaxis(np.asarray(x, np.float32).astype(ml_dtypes.bfloat16).astype(np.float64), axis, -1)
    blocks = v.reshape(v.shape[:-1] + (-1, 32))
    amax = np.abs(blocks).max(-1, keepdims=True)
    byte = np.maximum(np.where(amax > 0, np.frexp(amax)[1] - 1 + 127, 0) - down, 1)
    scale = np.exp2(byte - 127.0)
    codes = (blocks / scale).astype(np.float32).astype(dtype).astype(np.float64)
    return np.moveaxis((codes * scale).reshape(v.shape), -1, axis)


WIDE = False


def mx_kscale(k):
    if not WIDE:
        return np.ones(k)
    levels = np.array([10, -10, 5, -5, 0])
    a = np.random.permutation(np.resize(levels, k // 512 * 4)).reshape(k // 512, 4)
    idx = np.arange(k)
    return np.exp2(a[idx // 512, idx % 128 // 32])


BF16 = ml_dtypes.bfloat16


def bf(x):
    return np.asarray(x, np.float32).astype(BF16)


def f64(x):
    return np.asarray(x).astype(np.float64)


E2M1 = np.array([0.0, 0.5, 1.0, 1.5, 2.0, 3.0, 4.0, 6.0, -0.0, -0.5, -1.0, -1.5, -2.0, -3.0, -4.0, -6.0])


def pack_weight(w, fmt):
    k, n = w.shape
    w = f64(bf(w)).reshape(k // 32, 32, n)
    amax = np.abs(w).max(1)
    if fmt == "e4m3":
        byte = np.frexp(amax)[1] - 1 + 127 - 7
    else:
        mant, ex = np.frexp(amax / 6.0)
        byte = np.where(mant > 0.5, ex, ex - 1) + 127
    byte = np.clip(np.where(amax > 0, byte, 1), 1, 254)
    scaled = (w * np.exp2(127.0 - byte)[:, None, :]).reshape(k, n).astype(np.float32)
    by_word = np.ascontiguousarray(scaled.reshape(k // 512, 128, 4, n).transpose(0, 1, 3, 2))
    if fmt == "e4m3":
        words = by_word.astype(ml_dtypes.float8_e4m3fn).view(np.uint8)
    else:
        c = by_word.astype(ml_dtypes.float4_e2m1fn).view(np.uint8) & 0xF
        words = c[..., 0::2] | (c[..., 1::2] << 4)
    return np.ascontiguousarray(words), np.ascontiguousarray(byte.astype(np.uint8).reshape(k // 512, 16, n))


def unpack_weight(words, scales, fmt):
    g, p, n, _ = words.shape
    if fmt == "e4m3":
        vals = np.ascontiguousarray(words).view(ml_dtypes.float8_e4m3fn).astype(np.float64)
    else:
        nib = np.empty((g, p, n, 4), np.uint8)
        nib[..., 0::2] = words & 0xF
        nib[..., 1::2] = words >> 4
        vals = E2M1[nib]
    vals = vals * np.repeat(np.exp2(scales.astype(np.float64) - 127.0), 8, axis=1)[..., None]
    return vals.transpose(0, 1, 3, 2).reshape(g * 512, n)

def pack4(w):
    words, scales = pack_weight(w, "e2m1")
    return words.reshape(words.shape[0], 128, -1), scales


def unpack4(words, scales):
    return unpack_weight(words.reshape(words.shape[0], 128, -1, 2), scales, "e2m1")


B, S, C, H, D = 4, 512, 1024, 8, 128
E = H * D


def rope_tables():
    inv_freq = 1.0 / (10000.0 ** (np.arange(0, D, 2) / D))
    emb = np.repeat(np.outer(np.arange(S), inv_freq), 2, axis=1)
    return np.cos(emb), np.sin(emb)


def rope(t, cos, sin):
    tr = t[..., 0::2]
    ti = t[..., 1::2]
    t_rot = np.stack([-ti, tr], axis=-1).reshape(t.shape)
    return t * cos + t_rot * sin


def setup_inputs():
    s = mx_kscale(C)
    cos, sin = rope_tables()
    x = bf(np.random.standard_normal((B, S, C)) * s)
    Wq = np.random.standard_normal((E, C)) / np.sqrt(C) / s[None, :]
    Wq_words, Wq_scales = pack4(np.ascontiguousarray(Wq.T))
    bq = bf(np.random.standard_normal(E) * 0.1)
    return {"x": x,
            "cos": bf(cos), "sin": bf(sin),
            "Wq_words": Wq_words, "Wq_scales": Wq_scales,
            "bq": bq}


def reference(x, cos, sin, Wq_words, Wq_scales, bq):
    y = (mxq(f64(x), 2, "e4m3") @ unpack4(Wq_words, Wq_scales)) + f64(bq)
    q = y.reshape(B, S, H, D).transpose(0, 2, 1, 3)
    return np.maximum(rope(q, f64(cos), f64(sin)), 0.0)

@@ -1,0 +1,182 @@
+from contextlib import ExitStack
+
+import concourse.mybir as mybir
+from concourse.masks import make_identity
+
+F32 = mybir.dt.float32
+BF16 = mybir.dt.bfloat16
+I32 = mybir.dt.int32
+U8 = mybir.dt.uint8
+U32 = mybir.dt.uint32
+FP8X4 = mybir.dt.float8_e4m3fn_x4
+FP4X4 = mybir.dt.float4_e2m1fn_x4
+ADD = mybir.AluOpType.add
+MULT = mybir.AluOpType.mult
+RELU = mybir.ActivationFunctionType.Relu
+
+B, S, C, H, D = 4, 512, 1024, 8, 128
+E = H * D
+P = 128
+PACK = 4
+K_PASS = P * PACK
+PASSES = C // K_PASS
+TOKEN_TILES = S // P
+HEADS_PER_STORE = 2
+LAG = 1
+
+FLOPS = 2 * B * S * C * E
+
+
+def tile_lineartransformerblock_pa_kernel(tc, x, cos, sin, Wq_words, Wq_scales, bq, out):
+    nc = tc.nc
+    with ExitStack() as ctx:
+        const = ctx.enter_context(tc.tile_pool(name="const", bufs=1))
+        x_pool = ctx.enter_context(tc.tile_pool(name="x_pool", bufs=B))
+        stage = ctx.enter_context(tc.tile_pool(name="stage", bufs=2))
+        mx_pool = ctx.enter_context(tc.tile_pool(name="mx_pool", bufs=2))
+        prod_pool = ctx.enter_context(tc.tile_pool(name="prod_pool", bufs=3))
+        res_pool = ctx.enter_context(tc.tile_pool(name="res_pool", bufs=3))
+        psum_x = ctx.enter_context(tc.psum_pool(name="psum_x", bufs=2))
+        psum_acc = ctx.enter_context(tc.psum_pool(name="psum_acc", bufs=3))
+        psum_rot = ctx.enter_context(tc.psum_pool(name="psum_rot", bufs=3))
+
+        w_planes = const.tile([P, PASSES, E], U8, align_bytes=64)
+        nc.vector.memset(w_planes[:].bitcast(I32), 0)
+        x_tiles = []
+        for b in range(B):
+            x_sb = x_pool.tile([P, TOKEN_TILES, C], BF16)
+            x_tiles.append(x_sb)
+        nc.sync.dma_start(out=x_tiles[0][:], in_=x[0].rearrange("(p j) c -> p j c", j=TOKEN_TILES))
+        scale_words = Wq_scales.bitcast(I32)
+        for quadrant in range(4):
+            nc.sync.dma_start(
+                out=w_planes[32 * quadrant : 32 * quadrant + 4].bitcast(I32),
+                in_=scale_words[:, 4 * quadrant : 4 * quadrant + 4, :].rearrange("g r n -> r g n"),
+            )
+        w_words = const.tile([P, PASSES, 2 * E], U8, align_bytes=64)
+        nc.sync.dma_start(out=w_words[:].bitcast(I32), in_=Wq_words.bitcast(I32).rearrange("g p n -> p g n"))
+        for b in range(1, B):
+            nc.sync.dma_start(out=x_tiles[b][:], in_=x[b].rearrange("(p j) c -> p j c", j=TOKEN_TILES))
+
+        cos_rows = const.tile([P, TOKEN_TILES, D], BF16)
+        nc.scalar.dma_start(out=cos_rows[:], in_=cos.rearrange("(p j) d -> p j d", j=TOKEN_TILES))
+        sin_rows = const.tile([P, TOKEN_TILES, D], BF16)
+        nc.scalar.dma_start(out=sin_rows[:], in_=sin.rearrange("(p j) d -> p j d", j=TOKEN_TILES))
+        bq_rows = const.tile([P, P], BF16)
+        nc.vector.memset(bq_rows[:], 0.0)
+        nc.scalar.dma_start(out=bq_rows[0:H, :], in_=bq.rearrange("(h d) -> h d", d=D))
+
+        ident = const.tile([P, P], F32)
+        make_identity(nc, ident[:])
+        pair_swap = const.tile([P, P], F32)
+        ident_pairs = ident[:].rearrange("p (i e) -> p i e", e=2)
+        swap_pairs = pair_swap[:].rearrange("p (i e) -> p i e", e=2)
+        nc.vector.tensor_copy(out=swap_pairs[:, :, 0:1], in_=ident_pairs[:, :, 1:2])
+        nc.vector.tensor_copy(out=swap_pairs[:, :, 1:2], in_=ident_pairs[:, :, 0:1])
+
+        cos_f32 = const.tile([P, TOKEN_TILES, D], F32)
+        nc.vector.tensor_copy(out=cos_f32[:], in_=cos_rows[:])
+        partner_f32 = const.tile([P, TOKEN_TILES, D], F32)
+        sin_pairs = sin_rows[:].rearrange("p j (i e) -> p (j i) e", e=2)
+        partner_pairs = partner_f32[:].rearrange("p j (i e) -> p (j i) e", e=2)
+        nc.vector.tensor_copy(out=partner_pairs[:, :, 0:1], in_=sin_pairs[:, :, 1:2])
+        nc.vector.tensor_scalar_mul(out=partner_pairs[:, :, 1:2], in0=sin_pairs[:, :, 0:1], scalar1=-1.0)
+        bq_f32 = const.tile([P, P], F32)
+        nc.vector.tensor_copy(out=bq_f32[:], in_=bq_rows[:])
+
+        cos_t = const.tile([P, S], F32)
+        partner_t = const.tile([P, S], F32)
+        bias = const.tile([P, H], F32)
+        cos_ps = psum_x.tile([P, S], F32, tag="xt")
+        for j in range(TOKEN_TILES):
+            nc.tensor.transpose(cos_ps[:, j * P : (j + 1) * P], cos_f32[:, j, :], ident[:])
+        nc.vector.tensor_copy(out=cos_t[:], in_=cos_ps[:])
+        partner_ps = psum_x.tile([P, S], F32, tag="xt")
+        for j in range(TOKEN_TILES):
+            nc.tensor.transpose(partner_ps[:, j * P : (j + 1) * P], partner_f32[:, j, :], ident[:])
+        nc.vector.tensor_copy(out=partner_t[:], in_=partner_ps[:])
+        bias_ps = psum_x.tile([P, S], F32, tag="xt")
+        nc.tensor.transpose(bias_ps[:, 0:P], bq_f32[:], ident[:])
+        nc.vector.tensor_copy(out=bias[:], in_=bias_ps[:, 0:H])
+
+        def quantise_batch(b):
+            x_words = x_tiles[b][:].bitcast(F32)
+            x_codes = mx_pool.tile([P, PASSES, S], U32, align_bytes=64)
+            x_planes = mx_pool.tile([P, PASSES, S], U8, align_bytes=64)
+            for g in range(PASSES):
+                grouped = stage.tile([P, S * PACK], BF16, align_bytes=64)
+                grouped_words = grouped[:].bitcast(F32).rearrange("q (n u) -> q n u", u=2)
+                for half in range(2):
+                    xt = psum_x.tile([P, 2, 2 * P], F32, tag="xt")
+                    for u in range(2):
+                        for jj in range(2):
+                            nc.tensor.transpose(
+                                xt[:, u, jj * P : (jj + 1) * P],
+                                x_words[:, 2 * half + jj, 256 * g + u : 256 * (g + 1) : 2],
+                                ident[:],
+                            )
+                    nc.scalar.copy(
+                        out=grouped_words[:, 2 * P * half : 2 * P * (half + 1), :],
+                        in_=xt[:].rearrange("q u n -> q n u"),
+                    )
+                nc.vector.quantize_mx(
+                    out=x_codes[:, g, :].bitcast(FP8X4), scales=x_planes[:, g, :], in_=grouped[:]
+                )
+            return x_codes, x_planes
+
+        def project(x_codes, x_planes, h):
+            acc = psum_acc.tile([P, S], F32)
+            for g in range(PASSES):
+                nc.tensor.matmul_mx(
+                    out=acc[:],
+                    lhsT=w_words[:, g, 2 * D * h : 2 * D * (h + 1)].bitcast(FP4X4),
+                    lhsT_scale=w_planes[:, g, D * h : D * (h + 1)],
+                    rhs=x_codes[:, g, :].bitcast(FP8X4),
+                    rhs_scale=x_planes[:, g, :],
+                    start=(g == 0),
+                    stop=(g == PASSES - 1),
+                )
+            own = prod_pool.tile([P, S], F32)
+            nc.vector.scalar_tensor_tensor(
+                out=own[:], in0=acc[:], scalar=bias[:, h : h + 1], in1=cos_t[:], op0=ADD, op1=MULT
+            )
+            other = prod_pool.tile([P, S], F32)
+            nc.vector.scalar_tensor_tensor(
+                out=other[:], in0=acc[:], scalar=bias[:, h : h + 1], in1=partner_t[:], op0=ADD, op1=MULT
+            )
+            return own, other
+
+        def rotate(own, other, res_rows):
+            rot = psum_rot.tile([P, TOKEN_TILES, D], F32)
+            for j in range(TOKEN_TILES):
+                tokens = slice(j * P, (j + 1) * P)
+                nc.tensor.matmul(
+                    out=rot[:, j, :], lhsT=own[:, tokens], rhs=ident[:], is_transpose=True, start=True, stop=False
+                )
+                nc.tensor.matmul(
+                    out=rot[:, j, :], lhsT=other[:, tokens], rhs=pair_swap[:], is_transpose=True, start=False, stop=True
+                )
+            nc.scalar.activation(out=res_rows, in_=rot[:].rearrange("p j d -> p (j d)"), func=RELU)
+
+        units = [(b, h) for b in range(B) for h in range(H)]
+        mx_of_batch = {0: quantise_batch(0)}
+        products = {}
+        res_tiles = {}
+        for step in range(len(units) + LAG):
+            if step < len(units):
+                b, h = units[step]
+                if h == 0 and b + 1 < B:
+                    mx_of_batch[b + 1] = quantise_batch(b + 1)
+                products[step] = project(mx_of_batch[b][0], mx_of_batch[b][1], h)
+            if step >= LAG:
+                b, h = units[step - LAG]
+                slot = h % HEADS_PER_STORE
+                if slot == 0:
+                    res = res_pool.tile([P, HEADS_PER_STORE, TOKEN_TILES * D], F32)
+                    res_tiles[b] = res
+                rotate(products[step - LAG][0], products[step - LAG][1], res_tiles[b][:, slot, :])
+                if slot == HEADS_PER_STORE - 1:
+                    nc.sync.dma_start(
+                        out=out[b, h - slot : h + 1].rearrange("h (p j) d -> p h (j d)", j=TOKEN_TILES),
+                        in_=res_tiles[b][:],
+                    )

@@ -21,8 +21,10 @@ PACK = 4
 K_PASS = P * PACK
 PASSES = C // K_PASS
 TOKEN_TILES = S // P
-HEADS_PER_STORE = 2
-LAG = 1
+QUARTERS = 2 * PASSES
+GROUP = 2
+GROUPS = B * H // GROUP
+QUARTERS_AHEAD = QUARTERS + 1
 
 FLOPS = 2 * B * S * C * E
 
@@ -30,23 +32,37 @@ FLOPS = 2 * B * S * C * E
 def tile_lineartransformerblock_pa_kernel(tc, x, cos, sin, Wq_words, Wq_scales, bq, out):
     nc = tc.nc
     with ExitStack() as ctx:
+        ctx.enter_context(tc.manual_schedule())
         const = ctx.enter_context(tc.tile_pool(name="const", bufs=1))
-        x_pool = ctx.enter_context(tc.tile_pool(name="x_pool", bufs=B))
+        x_pool = ctx.enter_context(tc.tile_pool(name="x_pool", bufs=B * QUARTERS))
         stage = ctx.enter_context(tc.tile_pool(name="stage", bufs=2))
-        mx_pool = ctx.enter_context(tc.tile_pool(name="mx_pool", bufs=2))
-        prod_pool = ctx.enter_context(tc.tile_pool(name="prod_pool", bufs=3))
-        res_pool = ctx.enter_context(tc.tile_pool(name="res_pool", bufs=3))
+        mx_pool = ctx.enter_context(tc.tile_pool(name="mx_pool", bufs=2 * PASSES))
+        prod_pool = ctx.enter_context(tc.tile_pool(name="prod_pool", bufs=2 * GROUP))
+        res_pool = ctx.enter_context(tc.tile_pool(name="res_pool", bufs=3 * GROUP))
         psum_x = ctx.enter_context(tc.psum_pool(name="psum_x", bufs=2))
-        psum_acc = ctx.enter_context(tc.psum_pool(name="psum_acc", bufs=3))
-        psum_rot = ctx.enter_context(tc.psum_pool(name="psum_rot", bufs=3))
+        psum_acc = ctx.enter_context(tc.psum_pool(name="psum_acc", bufs=2 * GROUP))
+        psum_rot = ctx.enter_context(tc.psum_pool(name="psum_rot", bufs=GROUP))
 
         w_planes = const.tile([P, PASSES, E], U8, align_bytes=64)
         nc.vector.memset(w_planes[:].bitcast(I32), 0)
-        x_tiles = []
-        for b in range(B):
-            x_sb = x_pool.tile([P, TOKEN_TILES, C], BF16)
-            x_tiles.append(x_sb)
-        nc.sync.dma_start(out=x_tiles[0][:], in_=x[0].rearrange("(p j) c -> p j c", j=TOKEN_TILES))
+        bq_rows = const.tile([P, P], BF16)
+        nc.vector.memset(bq_rows[:], 0.0)
+
+        x_quarters = []
+
+        def load_quarter(q):
+            b, g, half = q // QUARTERS, (q % QUARTERS) // 2, q % 2
+            x_sb = x_pool.tile([P, 2, K_PASS], BF16)
+            nc.sync.dma_start(
+                out=x_sb[:],
+                in_=x[b].rearrange("(p j) c -> p j c", j=TOKEN_TILES)[
+                    :, 2 * half : 2 * half + 2, K_PASS * g : K_PASS * (g + 1)
+                ],
+            )
+            x_quarters.append(x_sb)
+
+        for q in range(QUARTERS):
+            load_quarter(q)
         scale_words = Wq_scales.bitcast(I32)
         for quadrant in range(4):
             nc.sync.dma_start(
@@ -55,15 +71,13 @@ def tile_lineartransformerblock_pa_kernel(tc, x, cos, sin, Wq_words, Wq_scales, 
             )
         w_words = const.tile([P, PASSES, 2 * E], U8, align_bytes=64)
         nc.sync.dma_start(out=w_words[:].bitcast(I32), in_=Wq_words.bitcast(I32).rearrange("g p n -> p g n"))
-        for b in range(1, B):
-            nc.sync.dma_start(out=x_tiles[b][:], in_=x[b].rearrange("(p j) c -> p j c", j=TOKEN_TILES))
+        for q in range(QUARTERS, B * QUARTERS):
+            load_quarter(q)
 
         cos_rows = const.tile([P, TOKEN_TILES, D], BF16)
         nc.scalar.dma_start(out=cos_rows[:], in_=cos.rearrange("(p j) d -> p j d", j=TOKEN_TILES))
         sin_rows = const.tile([P, TOKEN_TILES, D], BF16)
         nc.scalar.dma_start(out=sin_rows[:], in_=sin.rearrange("(p j) d -> p j d", j=TOKEN_TILES))
-        bq_rows = const.tile([P, P], BF16)
-        nc.vector.memset(bq_rows[:], 0.0)
         nc.scalar.dma_start(out=bq_rows[0:H, :], in_=bq.rearrange("(h d) -> h d", d=D))
 
         ident = const.tile([P, P], F32)
@@ -84,55 +98,60 @@ def tile_lineartransformerblock_pa_kernel(tc, x, cos, sin, Wq_words, Wq_scales, 
         bq_f32 = const.tile([P, P], F32)
         nc.vector.tensor_copy(out=bq_f32[:], in_=bq_rows[:])
 
+        grouped_of = {}
+        mx_of = {}
+
+        def transpose_quarter(q):
+            b, g, half = q // QUARTERS, (q % QUARTERS) // 2, q % 2
+            if half == 0:
+                grouped = stage.tile([P, S * PACK], BF16, align_bytes=64)
+                grouped_of[(b, g)] = grouped
+            x_words = x_quarters[q][:].bitcast(F32)
+            xt = psum_x.tile([P, 2, 2 * P], F32)
+            for u in range(2):
+                for jj in range(2):
+                    nc.tensor.transpose(xt[:, u, jj * P : (jj + 1) * P], x_words[:, jj, u : 2 * P : 2], ident[:])
+            grouped_words = grouped_of[(b, g)][:].bitcast(F32).rearrange("q (n u) -> q n u", u=2)
+            nc.scalar.copy(
+                out=grouped_words[:, 2 * P * half : 2 * P * (half + 1), :], in_=xt[:].rearrange("q u n -> q n u")
+            )
+            if half == 1:
+                x_codes = mx_pool.tile([P, S], U32, align_bytes=64)
+                x_planes = mx_pool.tile([P, S], U8, align_bytes=64)
+                nc.vector.quantize_mx(out=x_codes[:].bitcast(FP8X4), scales=x_planes[:], in_=grouped_of[(b, g)][:])
+                mx_of[(b, g)] = (x_codes, x_planes)
+
+        for q in range(QUARTERS):
+            transpose_quarter(q)
+
         cos_t = const.tile([P, S], F32)
         partner_t = const.tile([P, S], F32)
         bias = const.tile([P, H], F32)
-        cos_ps = psum_x.tile([P, S], F32, tag="xt")
+        cos_ps = psum_acc.tile([P, S], F32, tag="acc")
         for j in range(TOKEN_TILES):
             nc.tensor.transpose(cos_ps[:, j * P : (j + 1) * P], cos_f32[:, j, :], ident[:])
         nc.vector.tensor_copy(out=cos_t[:], in_=cos_ps[:])
-        partner_ps = psum_x.tile([P, S], F32, tag="xt")
+        partner_ps = psum_acc.tile([P, S], F32, tag="acc")
         for j in range(TOKEN_TILES):
             nc.tensor.transpose(partner_ps[:, j * P : (j + 1) * P], partner_f32[:, j, :], ident[:])
         nc.vector.tensor_copy(out=partner_t[:], in_=partner_ps[:])
-        bias_ps = psum_x.tile([P, S], F32, tag="xt")
+        bias_ps = psum_acc.tile([P, S], F32, tag="acc")
         nc.tensor.transpose(bias_ps[:, 0:P], bq_f32[:], ident[:])
         nc.vector.tensor_copy(out=bias[:], in_=bias_ps[:, 0:H])
 
-        def quantise_batch(b):
-            x_words = x_tiles[b][:].bitcast(F32)
-            x_codes = mx_pool.tile([P, PASSES, S], U32, align_bytes=64)
-            x_planes = mx_pool.tile([P, PASSES, S], U8, align_bytes=64)
-            for g in range(PASSES):
-                grouped = stage.tile([P, S * PACK], BF16, align_bytes=64)
-                grouped_words = grouped[:].bitcast(F32).rearrange("q (n u) -> q n u", u=2)
-                for half in range(2):
-                    xt = psum_x.tile([P, 2, 2 * P], F32, tag="xt")
-                    for u in range(2):
-                        for jj in range(2):
-                            nc.tensor.transpose(
-                                xt[:, u, jj * P : (jj + 1) * P],
-                                x_words[:, 2 * half + jj, 256 * g + u : 256 * (g + 1) : 2],
-                                ident[:],
-                            )
-                    nc.scalar.copy(
-                        out=grouped_words[:, 2 * P * half : 2 * P * (half + 1), :],
-                        in_=xt[:].rearrange("q u n -> q n u"),
-                    )
-                nc.vector.quantize_mx(
-                    out=x_codes[:, g, :].bitcast(FP8X4), scales=x_planes[:, g, :], in_=grouped[:]
-                )
-            return x_codes, x_planes
+        for q in range(QUARTERS, QUARTERS_AHEAD):
+            transpose_quarter(q)
 
-        def project(x_codes, x_planes, h):
-            acc = psum_acc.tile([P, S], F32)
+        def project(b, h):
+            acc = psum_acc.tile([P, S], F32, tag="acc")
             for g in range(PASSES):
+                x_codes, x_planes = mx_of[(b, g)]
                 nc.tensor.matmul_mx(
                     out=acc[:],
                     lhsT=w_words[:, g, 2 * D * h : 2 * D * (h + 1)].bitcast(FP4X4),
                     lhsT_scale=w_planes[:, g, D * h : D * (h + 1)],
-                    rhs=x_codes[:, g, :].bitcast(FP8X4),
-                    rhs_scale=x_planes[:, g, :],
+                    rhs=x_codes[:].bitcast(FP8X4),
+                    rhs_scale=x_planes[:],
                     start=(g == 0),
                     stop=(g == PASSES - 1),
                 )
@@ -146,7 +165,7 @@ def tile_lineartransformerblock_pa_kernel(tc, x, cos, sin, Wq_words, Wq_scales, 
             )
             return own, other
 
-        def rotate(own, other, res_rows):
+        def rotate(b, h, own, other):
             rot = psum_rot.tile([P, TOKEN_TILES, D], F32)
             for j in range(TOKEN_TILES):
                 tokens = slice(j * P, (j + 1) * P)
@@ -156,27 +175,17 @@ def tile_lineartransformerblock_pa_kernel(tc, x, cos, sin, Wq_words, Wq_scales, 
                 nc.tensor.matmul(
                     out=rot[:, j, :], lhsT=other[:, tokens], rhs=pair_swap[:], is_transpose=True, start=False, stop=True
                 )
-            nc.scalar.activation(out=res_rows, in_=rot[:].rearrange("p j d -> p (j d)"), func=RELU)
+            res = res_pool.tile([P, TOKEN_TILES * D], F32)
+            nc.scalar.activation(out=res[:], in_=rot[:].rearrange("p j d -> p (j d)"), func=RELU)
+            nc.sync.dma_start(out=out[b, h].rearrange("(p j) d -> p (j d)", j=TOKEN_TILES), in_=res[:])
 
-        units = [(b, h) for b in range(B) for h in range(H)]
-        mx_of_batch = {0: quantise_batch(0)}
         products = {}
-        res_tiles = {}
-        for step in range(len(units) + LAG):
-            if step < len(units):
-                b, h = units[step]
-                if h == 0 and b + 1 < B:
-                    mx_of_batch[b + 1] = quantise_batch(b + 1)
-                products[step] = project(mx_of_batch[b][0], mx_of_batch[b][1], h)
-            if step >= LAG:
-                b, h = units[step - LAG]
-                slot = h % HEADS_PER_STORE
-                if slot == 0:
-                    res = res_pool.tile([P, HEADS_PER_STORE, TOKEN_TILES * D], F32)
-                    res_tiles[b] = res
-                rotate(products[step - LAG][0], products[step - LAG][1], res_tiles[b][:, slot, :])
-                if slot == HEADS_PER_STORE - 1:
-                    nc.sync.dma_start(
-                        out=out[b, h - slot : h + 1].rearrange("h (p j) d -> p h (j d)", j=TOKEN_TILES),
-                        in_=res_tiles[b][:],
-                    )
+        for step in range(GROUPS + 1):
+            if step < GROUPS:
+                for unit in range(GROUP * step, GROUP * (step + 1)):
+                    products[unit] = project(unit // H, unit % H)
+            if step >= 1:
+                for unit in range(GROUP * (step - 1), GROUP * step):
+                    rotate(unit // H, unit % H, products[unit][0], products[unit][1])
+            if step + QUARTERS_AHEAD < B * QUARTERS:
+                transpose_quarter(step + QUARTERS_AHEAD)

@@ -35,6 +35,7 @@ def tile_lineartransformerblock_pa_kernel(tc, x, cos, sin, Wq_words, Wq_scales, 
         ctx.enter_context(tc.manual_schedule())
         const = ctx.enter_context(tc.tile_pool(name="const", bufs=1))
         x_pool = ctx.enter_context(tc.tile_pool(name="x_pool", bufs=B * QUARTERS))
+        sort_pool = ctx.enter_context(tc.tile_pool(name="sort_pool", bufs=3))
         stage = ctx.enter_context(tc.tile_pool(name="stage", bufs=2))
         mx_pool = ctx.enter_context(tc.tile_pool(name="mx_pool", bufs=2 * PASSES))
         prod_pool = ctx.enter_context(tc.tile_pool(name="prod_pool", bufs=2 * GROUP))
@@ -98,19 +99,24 @@ def tile_lineartransformerblock_pa_kernel(tc, x, cos, sin, Wq_words, Wq_scales, 
         bq_f32 = const.tile([P, P], F32)
         nc.vector.tensor_copy(out=bq_f32[:], in_=bq_rows[:])
 
+        sorted_of = {}
         grouped_of = {}
         mx_of = {}
+
+        def sort_quarter(q):
+            x_sorted = sort_pool.tile([P, 2, 2, P], F32)
+            nc.scalar.copy(out=x_sorted[:], in_=x_quarters[q][:].bitcast(F32).rearrange("p j (q u) -> p j u q", u=2))
+            sorted_of[q] = x_sorted
 
         def transpose_quarter(q):
             b, g, half = q // QUARTERS, (q % QUARTERS) // 2, q % 2
             if half == 0:
                 grouped = stage.tile([P, S * PACK], BF16, align_bytes=64)
                 grouped_of[(b, g)] = grouped
-            x_words = x_quarters[q][:].bitcast(F32)
             xt = psum_x.tile([P, 2, 2 * P], F32)
             for u in range(2):
                 for jj in range(2):
-                    nc.tensor.transpose(xt[:, u, jj * P : (jj + 1) * P], x_words[:, jj, u : 2 * P : 2], ident[:])
+                    nc.tensor.transpose(xt[:, u, jj * P : (jj + 1) * P], sorted_of[q][:, jj, u, :], ident[:])
             grouped_words = grouped_of[(b, g)][:].bitcast(F32).rearrange("q (n u) -> q n u", u=2)
             nc.scalar.copy(
                 out=grouped_words[:, 2 * P * half : 2 * P * (half + 1), :], in_=xt[:].rearrange("q u n -> q n u")
@@ -121,7 +127,9 @@ def tile_lineartransformerblock_pa_kernel(tc, x, cos, sin, Wq_words, Wq_scales, 
                 nc.vector.quantize_mx(out=x_codes[:].bitcast(FP8X4), scales=x_planes[:], in_=grouped_of[(b, g)][:])
                 mx_of[(b, g)] = (x_codes, x_planes)
 
+        sort_quarter(0)
         for q in range(QUARTERS):
+            sort_quarter(q + 1)
             transpose_quarter(q)
 
         cos_t = const.tile([P, S], F32)
@@ -181,6 +189,8 @@ def tile_lineartransformerblock_pa_kernel(tc, x, cos, sin, Wq_words, Wq_scales, 
 
         products = {}
         for step in range(GROUPS + 1):
+            if step + QUARTERS_AHEAD < B * QUARTERS:
+                sort_quarter(step + QUARTERS_AHEAD)
             if step < GROUPS:
                 for unit in range(GROUP * step, GROUP * (step + 1)):
                     products[unit] = project(unit // H, unit % H)

@@ -22,8 +22,10 @@ K_PASS = P * PACK
 PASSES = C // K_PASS
 TOKEN_TILES = S // P
 QUARTERS = 2 * PASSES
-GROUP = 2
-GROUPS = B * H // GROUP
+ROW_HEADS = 4
+COL_HEADS = H - ROW_HEADS
+ROW_WIDTH = ROW_HEADS * D
+SLOTS = B * COL_HEADS
 QUARTERS_AHEAD = QUARTERS + 1
 
 FLOPS = 2 * B * S * C * E
@@ -38,11 +40,12 @@ def tile_lineartransformerblock_pa_kernel(tc, x, cos, sin, Wq_words, Wq_scales, 
         sort_pool = ctx.enter_context(tc.tile_pool(name="sort_pool", bufs=3))
         stage = ctx.enter_context(tc.tile_pool(name="stage", bufs=2))
         mx_pool = ctx.enter_context(tc.tile_pool(name="mx_pool", bufs=2 * PASSES))
-        prod_pool = ctx.enter_context(tc.tile_pool(name="prod_pool", bufs=2 * GROUP))
-        res_pool = ctx.enter_context(tc.tile_pool(name="res_pool", bufs=3 * GROUP))
+        prod_pool = ctx.enter_context(tc.tile_pool(name="prod_pool", bufs=3))
+        sum_pool = ctx.enter_context(tc.tile_pool(name="sum_pool", bufs=3))
+        res_pool = ctx.enter_context(tc.tile_pool(name="res_pool", bufs=4))
         psum_x = ctx.enter_context(tc.psum_pool(name="psum_x", bufs=2))
-        psum_acc = ctx.enter_context(tc.psum_pool(name="psum_acc", bufs=2 * GROUP))
-        psum_rot = ctx.enter_context(tc.psum_pool(name="psum_rot", bufs=GROUP))
+        psum_acc = ctx.enter_context(tc.psum_pool(name="psum_acc", bufs=4))
+        psum_rot = ctx.enter_context(tc.psum_pool(name="psum_rot", bufs=2))
 
         w_planes = const.tile([P, PASSES, E], U8, align_bytes=64)
         nc.vector.memset(w_planes[:].bitcast(I32), 0)
@@ -91,11 +94,19 @@ def tile_lineartransformerblock_pa_kernel(tc, x, cos, sin, Wq_words, Wq_scales, 
 
         cos_f32 = const.tile([P, TOKEN_TILES, D], F32)
         nc.vector.tensor_copy(out=cos_f32[:], in_=cos_rows[:])
-        partner_f32 = const.tile([P, TOKEN_TILES, D], F32)
         sin_pairs = sin_rows[:].rearrange("p j (i e) -> p (j i) e", e=2)
+        partner_f32 = const.tile([P, TOKEN_TILES, D], F32)
         partner_pairs = partner_f32[:].rearrange("p j (i e) -> p (j i) e", e=2)
         nc.vector.tensor_copy(out=partner_pairs[:, :, 0:1], in_=sin_pairs[:, :, 1:2])
         nc.vector.tensor_scalar_mul(out=partner_pairs[:, :, 1:2], in0=sin_pairs[:, :, 0:1], scalar1=-1.0)
+        signed_rows = const.tile([P, TOKEN_TILES, D], BF16)
+        signed_pairs = signed_rows[:].rearrange("p j (i e) -> p (j i) e", e=2)
+        nc.gpsimd.tensor_scalar(
+            out=signed_pairs[:, :, 0:1], in0=sin_pairs[:, :, 0:1], scalar1=-1.0, scalar2=0.0, op0=MULT, op1=ADD
+        )
+        nc.gpsimd.tensor_scalar(
+            out=signed_pairs[:, :, 1:2], in0=sin_pairs[:, :, 1:2], scalar1=1.0, scalar2=0.0, op0=MULT, op1=ADD
+        )
         bq_f32 = const.tile([P, P], F32)
         nc.vector.tensor_copy(out=bq_f32[:], in_=bq_rows[:])
 
@@ -132,9 +143,12 @@ def tile_lineartransformerblock_pa_kernel(tc, x, cos, sin, Wq_words, Wq_scales, 
             sort_quarter(q + 1)
             transpose_quarter(q)
 
-        cos_t = const.tile([P, S], F32)
-        partner_t = const.tile([P, S], F32)
+        cos_t = const.tile([P, S], BF16)
+        partner_t = const.tile([P, S], BF16)
         bias = const.tile([P, H], F32)
+        bias_ps = psum_acc.tile([P, S], F32, tag="acc")
+        nc.tensor.transpose(bias_ps[:, 0:P], bq_f32[:], ident[:])
+        nc.vector.tensor_copy(out=bias[:], in_=bias_ps[:, 0:H])
         cos_ps = psum_acc.tile([P, S], F32, tag="acc")
         for j in range(TOKEN_TILES):
             nc.tensor.transpose(cos_ps[:, j * P : (j + 1) * P], cos_f32[:, j, :], ident[:])
@@ -143,14 +157,36 @@ def tile_lineartransformerblock_pa_kernel(tc, x, cos, sin, Wq_words, Wq_scales, 
         for j in range(TOKEN_TILES):
             nc.tensor.transpose(partner_ps[:, j * P : (j + 1) * P], partner_f32[:, j, :], ident[:])
         nc.vector.tensor_copy(out=partner_t[:], in_=partner_ps[:])
-        bias_ps = psum_acc.tile([P, S], F32, tag="acc")
-        nc.tensor.transpose(bias_ps[:, 0:P], bq_f32[:], ident[:])
-        nc.vector.tensor_copy(out=bias[:], in_=bias_ps[:, 0:H])
+
+        own_diag = const.tile([P, ROW_HEADS, D], BF16)
+        swap_diag = const.tile([P, ROW_HEADS, D], BF16)
+        for h in range(ROW_HEADS):
+            nc.gpsimd.tensor_scalar(
+                out=own_diag[:, h, :], in0=ident[:], scalar1=bias[:, h : h + 1], scalar2=0.0, op0=MULT, op1=ADD
+            )
+            nc.gpsimd.tensor_scalar(
+                out=swap_diag[:, h, :], in0=pair_swap[:], scalar1=bias[:, h : h + 1], scalar2=0.0, op0=MULT, op1=ADD
+            )
+        roped_bias = const.tile([P, TOKEN_TILES, ROW_WIDTH], F32)
+        for j in range(TOKEN_TILES):
+            rb_ps = psum_acc.tile([P, S], F32, tag="acc")
+            tokens = slice(j * P, (j + 1) * P)
+            nc.tensor.matmul(
+                out=rb_ps[:], lhsT=cos_t[:, tokens], rhs=own_diag[:].rearrange("p h d -> p (h d)"), start=True, stop=False
+            )
+            nc.tensor.matmul(
+                out=rb_ps[:],
+                lhsT=partner_t[:, tokens],
+                rhs=swap_diag[:].rearrange("p h d -> p (h d)"),
+                start=False,
+                stop=True,
+            )
+            nc.vector.tensor_copy(out=roped_bias[:, j, :], in_=rb_ps[:])
 
         for q in range(QUARTERS, QUARTERS_AHEAD):
             transpose_quarter(q)
 
-        def project(b, h):
+        def project_columns(b, h):
             acc = psum_acc.tile([P, S], F32, tag="acc")
             for g in range(PASSES):
                 x_codes, x_planes = mx_of[(b, g)]
@@ -187,15 +223,67 @@ def tile_lineartransformerblock_pa_kernel(tc, x, cos, sin, Wq_words, Wq_scales, 
             nc.scalar.activation(out=res[:], in_=rot[:].rearrange("p j d -> p (j d)"), func=RELU)
             nc.sync.dma_start(out=out[b, h].rearrange("(p j) d -> p (j d)", j=TOKEN_TILES), in_=res[:])
 
+        def project_rows(b, j):
+            acc = psum_acc.tile([P, S], F32, tag="acc")
+            tokens = slice(j * P, (j + 1) * P)
+            for g in range(PASSES):
+                x_codes, x_planes = mx_of[(b, g)]
+                nc.tensor.matmul_mx(
+                    out=acc[:],
+                    lhsT=x_codes[:, tokens].bitcast(FP8X4),
+                    lhsT_scale=x_planes[:, tokens],
+                    rhs=w_words[:, g, 0 : 2 * ROW_WIDTH].bitcast(FP4X4),
+                    rhs_scale=w_planes[:, g, 0:ROW_WIDTH],
+                    start=(g == 0),
+                    stop=(g == PASSES - 1),
+                )
+            straight = prod_pool.tile([P, ROW_HEADS, D], F32)
+            nc.vector.tensor_tensor(
+                out=straight[:],
+                in0=acc[:].rearrange("p (h d) -> p h d", h=ROW_HEADS),
+                in1=cos_rows[:, j, :].unsqueeze(1).to_broadcast([P, ROW_HEADS, D]),
+                op=MULT,
+            )
+            crossed = prod_pool.tile([P, ROW_HEADS, D // 2, 2], F32)
+            nc.vector.tensor_tensor(
+                out=crossed[:],
+                in0=acc[:].rearrange("p (h i e) -> p h i e", h=ROW_HEADS, e=2)[:, :, :, ::-1],
+                in1=signed_rows[:, j, :]
+                .rearrange("p (i e) -> p i e", e=2)
+                .unsqueeze(1)
+                .to_broadcast([P, ROW_HEADS, D // 2, 2]),
+                op=MULT,
+            )
+            biased = sum_pool.tile([P, ROW_WIDTH], F32)
+            nc.gpsimd.tensor_tensor(
+                out=biased[:], in0=straight[:].rearrange("p h d -> p (h d)"), in1=roped_bias[:, j, :], op=ADD
+            )
+            total = sum_pool.tile([P, ROW_WIDTH], F32)
+            nc.gpsimd.tensor_tensor(
+                out=total[:], in0=biased[:], in1=crossed[:].rearrange("p h i e -> p (h i e)"), op=ADD
+            )
+            return total
+
+        def finish_rows(b, j, total):
+            res_rows = res_pool.tile([P, ROW_HEADS, D], F32)
+            nc.scalar.activation(out=res_rows[:].rearrange("p h d -> p (h d)"), in_=total[:], func=RELU)
+            nc.sync.dma_start(
+                out=out[b, 0:ROW_HEADS].rearrange("h (p j) d -> p j h d", j=TOKEN_TILES)[:, j], in_=res_rows[:]
+            )
+
         products = {}
-        for step in range(GROUPS + 1):
-            if step + QUARTERS_AHEAD < B * QUARTERS:
-                sort_quarter(step + QUARTERS_AHEAD)
-            if step < GROUPS:
-                for unit in range(GROUP * step, GROUP * (step + 1)):
-                    products[unit] = project(unit // H, unit % H)
-            if step >= 1:
-                for unit in range(GROUP * (step - 1), GROUP * step):
-                    rotate(unit // H, unit % H, products[unit][0], products[unit][1])
-            if step + QUARTERS_AHEAD < B * QUARTERS:
-                transpose_quarter(step + QUARTERS_AHEAD)
+        totals = {}
+        for slot in range(SLOTS + 2):
+            if slot + QUARTERS_AHEAD < B * QUARTERS:
+                sort_quarter(slot + QUARTERS_AHEAD)
+            if slot < SLOTS:
+                products[slot] = project_columns(slot // COL_HEADS, ROW_HEADS + slot % COL_HEADS)
+                totals[slot] = project_rows(slot // TOKEN_TILES, slot % TOKEN_TILES)
+            if 1 <= slot <= SLOTS:
+                before = slot - 1
+                rotate(before // COL_HEADS, ROW_HEADS + before % COL_HEADS, products[before][0], products[before][1])
+            if slot >= 2:
+                before = slot - 2
+                finish_rows(before // TOKEN_TILES, before % TOKEN_TILES, totals[before])
+            if slot + QUARTERS_AHEAD < B * QUARTERS:
+                transpose_quarter(slot + QUARTERS_AHEAD)

@@ -22,13 +22,34 @@ K_PASS = P * PACK
 PASSES = C // K_PASS
 TOKEN_TILES = S // P
 QUARTERS = 2 * PASSES
+HALF = S // 2
 ROW_HEADS = 4
-COL_HEADS = H - ROW_HEADS
 ROW_WIDTH = ROW_HEADS * D
-SLOTS = B * COL_HEADS
-QUARTERS_AHEAD = QUARTERS + 1
+ROW_BATCHES = 3
+ROW_LAG = 4
+UNSORTED = QUARTERS
 
 FLOPS = 2 * B * S * C * E
+
+
+def unit_slots():
+    slots = [
+        [("row", 0, 0), ("row", 0, 1)],
+        [("col", 0, 4), ("row", 0, 2)],
+        [("col", 0, 5), ("row", 0, 3)],
+        [("col", 0, 6), ("col", 0, 7)],
+    ]
+    for b in range(1, B):
+        for i in range(4):
+            first = ("row", b, i) if b < ROW_BATCHES else ("col", b, i)
+            slots.append([("col", b, ROW_HEADS + i), first])
+    return slots
+
+
+def quarters_of_slot(slot):
+    if slot < 3:
+        return [2 * slot + 2, 2 * slot + 3]
+    return [slot + 5] if slot + 5 < B * QUARTERS else []
 
 
 def tile_lineartransformerblock_pa_kernel(tc, x, cos, sin, Wq_words, Wq_scales, bq, out):
@@ -38,10 +59,10 @@ def tile_lineartransformerblock_pa_kernel(tc, x, cos, sin, Wq_words, Wq_scales, 
         const = ctx.enter_context(tc.tile_pool(name="const", bufs=1))
         x_pool = ctx.enter_context(tc.tile_pool(name="x_pool", bufs=B * QUARTERS))
         sort_pool = ctx.enter_context(tc.tile_pool(name="sort_pool", bufs=3))
-        stage = ctx.enter_context(tc.tile_pool(name="stage", bufs=2))
+        stage = ctx.enter_context(tc.tile_pool(name="stage", bufs=4))
         mx_pool = ctx.enter_context(tc.tile_pool(name="mx_pool", bufs=2 * PASSES))
-        prod_pool = ctx.enter_context(tc.tile_pool(name="prod_pool", bufs=3))
-        sum_pool = ctx.enter_context(tc.tile_pool(name="sum_pool", bufs=3))
+        prod_pool = ctx.enter_context(tc.tile_pool(name="prod_pool", bufs=4))
+        row_pool = ctx.enter_context(tc.tile_pool(name="row_pool", bufs=6))
         res_pool = ctx.enter_context(tc.tile_pool(name="res_pool", bufs=4))
         psum_x = ctx.enter_context(tc.psum_pool(name="psum_x", bufs=2))
         psum_acc = ctx.enter_context(tc.psum_pool(name="psum_acc", bufs=4))
@@ -55,7 +76,7 @@ def tile_lineartransformerblock_pa_kernel(tc, x, cos, sin, Wq_words, Wq_scales, 
         x_quarters = []
 
         def load_quarter(q):
-            b, g, half = q // QUARTERS, (q % QUARTERS) // 2, q % 2
+            b, half, g = q // QUARTERS, (q % QUARTERS) // 2, q % 2
             x_sb = x_pool.tile([P, 2, K_PASS], BF16)
             nc.sync.dma_start(
                 out=x_sb[:],
@@ -65,38 +86,45 @@ def tile_lineartransformerblock_pa_kernel(tc, x, cos, sin, Wq_words, Wq_scales, 
             )
             x_quarters.append(x_sb)
 
-        for q in range(QUARTERS):
-            load_quarter(q)
+        w_words = const.tile([P, PASSES, 2 * E], U8, align_bytes=64)
+        w_words_i32 = w_words[:].bitcast(I32)
+        w_source_i32 = Wq_words.bitcast(I32).rearrange("g p n -> p g n")
+        row_words = ROW_WIDTH // 2
         scale_words = Wq_scales.bitcast(I32)
+
+        load_quarter(0)
+        load_quarter(1)
         for quadrant in range(4):
             nc.sync.dma_start(
                 out=w_planes[32 * quadrant : 32 * quadrant + 4].bitcast(I32),
                 in_=scale_words[:, 4 * quadrant : 4 * quadrant + 4, :].rearrange("g r n -> r g n"),
             )
-        w_words = const.tile([P, PASSES, 2 * E], U8, align_bytes=64)
-        nc.sync.dma_start(out=w_words[:].bitcast(I32), in_=Wq_words.bitcast(I32).rearrange("g p n -> p g n"))
+        nc.sync.dma_start(out=w_words_i32[:, :, 0:row_words], in_=w_source_i32[:, :, 0:row_words])
+        load_quarter(2)
+        load_quarter(3)
+        nc.sync.dma_start(out=w_words_i32[:, :, row_words:], in_=w_source_i32[:, :, row_words:])
         for q in range(QUARTERS, B * QUARTERS):
             load_quarter(q)
 
-        cos_rows = const.tile([P, TOKEN_TILES, D], BF16)
-        nc.scalar.dma_start(out=cos_rows[:], in_=cos.rearrange("(p j) d -> p j d", j=TOKEN_TILES))
+        nc.scalar.dma_start(out=bq_rows[0:H, :], in_=bq.rearrange("(h d) -> h d", d=D))
         sin_rows = const.tile([P, TOKEN_TILES, D], BF16)
         nc.scalar.dma_start(out=sin_rows[:], in_=sin.rearrange("(p j) d -> p j d", j=TOKEN_TILES))
-        nc.scalar.dma_start(out=bq_rows[0:H, :], in_=bq.rearrange("(h d) -> h d", d=D))
+        cos_rows = const.tile([P, TOKEN_TILES, D], BF16)
+        nc.scalar.dma_start(out=cos_rows[:], in_=cos.rearrange("(p j) d -> p j d", j=TOKEN_TILES))
 
         ident = const.tile([P, P], F32)
         make_identity(nc, ident[:])
+        ident_bf = const.tile([P, P], BF16)
+        nc.vector.tensor_copy(out=ident_bf[:], in_=ident[:])
         pair_swap = const.tile([P, P], F32)
         ident_pairs = ident[:].rearrange("p (i e) -> p i e", e=2)
         swap_pairs = pair_swap[:].rearrange("p (i e) -> p i e", e=2)
         nc.vector.tensor_copy(out=swap_pairs[:, :, 0:1], in_=ident_pairs[:, :, 1:2])
         nc.vector.tensor_copy(out=swap_pairs[:, :, 1:2], in_=ident_pairs[:, :, 0:1])
 
-        cos_f32 = const.tile([P, TOKEN_TILES, D], F32)
-        nc.vector.tensor_copy(out=cos_f32[:], in_=cos_rows[:])
         sin_pairs = sin_rows[:].rearrange("p j (i e) -> p (j i) e", e=2)
-        partner_f32 = const.tile([P, TOKEN_TILES, D], F32)
-        partner_pairs = partner_f32[:].rearrange("p j (i e) -> p (j i) e", e=2)
+        partner_rows = const.tile([P, TOKEN_TILES, D], BF16)
+        partner_pairs = partner_rows[:].rearrange("p j (i e) -> p (j i) e", e=2)
         nc.vector.tensor_copy(out=partner_pairs[:, :, 0:1], in_=sin_pairs[:, :, 1:2])
         nc.vector.tensor_scalar_mul(out=partner_pairs[:, :, 1:2], in0=sin_pairs[:, :, 0:1], scalar1=-1.0)
         signed_rows = const.tile([P, TOKEN_TILES, D], BF16)
@@ -107,8 +135,16 @@ def tile_lineartransformerblock_pa_kernel(tc, x, cos, sin, Wq_words, Wq_scales, 
         nc.gpsimd.tensor_scalar(
             out=signed_pairs[:, :, 1:2], in0=sin_pairs[:, :, 1:2], scalar1=1.0, scalar2=0.0, op0=MULT, op1=ADD
         )
-        bq_f32 = const.tile([P, P], F32)
-        nc.vector.tensor_copy(out=bq_f32[:], in_=bq_rows[:])
+
+        bias = const.tile([P, H], F32)
+        bias_ps = psum_rot.tile([P, 2 * S], BF16, tag="rot")
+        nc.tensor.transpose(bias_ps[:, 0:P], bq_rows[:], ident_bf[:])
+        nc.scalar.copy(out=bias[:], in_=bias_ps[:, 0:H])
+        own_diag = const.tile([P, ROW_HEADS, D], BF16)
+        swap_diag = const.tile([P, ROW_HEADS, D], BF16)
+        for h in range(ROW_HEADS):
+            nc.vector.tensor_scalar_mul(out=own_diag[:, h, :], in0=ident[:], scalar1=bias[:, h : h + 1])
+            nc.vector.tensor_scalar_mul(out=swap_diag[:, h, :], in0=pair_swap[:], scalar1=bias[:, h : h + 1])
 
         sorted_of = {}
         grouped_of = {}
@@ -117,59 +153,54 @@ def tile_lineartransformerblock_pa_kernel(tc, x, cos, sin, Wq_words, Wq_scales, 
         def sort_quarter(q):
             x_sorted = sort_pool.tile([P, 2, 2, P], F32)
             nc.scalar.copy(out=x_sorted[:], in_=x_quarters[q][:].bitcast(F32).rearrange("p j (q u) -> p j u q", u=2))
-            sorted_of[q] = x_sorted
+            sorted_of[q] = x_sorted[:]
 
-        def transpose_quarter(q):
-            b, g, half = q // QUARTERS, (q % QUARTERS) // 2, q % 2
-            if half == 0:
-                grouped = stage.tile([P, S * PACK], BF16, align_bytes=64)
-                grouped_of[(b, g)] = grouped
+        def turn_quarter(q):
+            if q < UNSORTED:
+                words = x_quarters[q][:].bitcast(F32).rearrange("p j (q u) -> p j u q", u=2)
+            else:
+                words = sorted_of[q]
             xt = psum_x.tile([P, 2, 2 * P], F32)
             for u in range(2):
                 for jj in range(2):
-                    nc.tensor.transpose(xt[:, u, jj * P : (jj + 1) * P], sorted_of[q][:, jj, u, :], ident[:])
-            grouped_words = grouped_of[(b, g)][:].bitcast(F32).rearrange("q (n u) -> q n u", u=2)
+                    nc.tensor.transpose(xt[:, u, jj * P : (jj + 1) * P], words[:, jj, u, :], ident[:])
+            grouped = stage.tile([P, HALF * PACK], BF16, align_bytes=64)
             nc.scalar.copy(
-                out=grouped_words[:, 2 * P * half : 2 * P * (half + 1), :], in_=xt[:].rearrange("q u n -> q n u")
+                out=grouped[:].bitcast(F32).rearrange("q (n u) -> q n u", u=2), in_=xt[:].rearrange("q u n -> q n u")
             )
-            if half == 1:
+            grouped_of[q] = grouped
+
+        def quantise_quarter(q):
+            b, half, g = q // QUARTERS, (q % QUARTERS) // 2, q % 2
+            if half == 0:
                 x_codes = mx_pool.tile([P, S], U32, align_bytes=64)
                 x_planes = mx_pool.tile([P, S], U8, align_bytes=64)
-                nc.vector.quantize_mx(out=x_codes[:].bitcast(FP8X4), scales=x_planes[:], in_=grouped_of[(b, g)][:])
                 mx_of[(b, g)] = (x_codes, x_planes)
-
-        sort_quarter(0)
-        for q in range(QUARTERS):
-            sort_quarter(q + 1)
-            transpose_quarter(q)
-
-        cos_t = const.tile([P, S], BF16)
-        partner_t = const.tile([P, S], BF16)
-        bias = const.tile([P, H], F32)
-        bias_ps = psum_acc.tile([P, S], F32, tag="acc")
-        nc.tensor.transpose(bias_ps[:, 0:P], bq_f32[:], ident[:])
-        nc.vector.tensor_copy(out=bias[:], in_=bias_ps[:, 0:H])
-        cos_ps = psum_acc.tile([P, S], F32, tag="acc")
-        for j in range(TOKEN_TILES):
-            nc.tensor.transpose(cos_ps[:, j * P : (j + 1) * P], cos_f32[:, j, :], ident[:])
-        nc.vector.tensor_copy(out=cos_t[:], in_=cos_ps[:])
-        partner_ps = psum_acc.tile([P, S], F32, tag="acc")
-        for j in range(TOKEN_TILES):
-            nc.tensor.transpose(partner_ps[:, j * P : (j + 1) * P], partner_f32[:, j, :], ident[:])
-        nc.vector.tensor_copy(out=partner_t[:], in_=partner_ps[:])
-
-        own_diag = const.tile([P, ROW_HEADS, D], BF16)
-        swap_diag = const.tile([P, ROW_HEADS, D], BF16)
-        for h in range(ROW_HEADS):
-            nc.gpsimd.tensor_scalar(
-                out=own_diag[:, h, :], in0=ident[:], scalar1=bias[:, h : h + 1], scalar2=0.0, op0=MULT, op1=ADD
+            x_codes, x_planes = mx_of[(b, g)]
+            tokens = slice(HALF * half, HALF * (half + 1))
+            nc.vector.quantize_mx(
+                out=x_codes[:, tokens].bitcast(FP8X4), scales=x_planes[:, tokens], in_=grouped_of[q][:]
             )
-            nc.gpsimd.tensor_scalar(
-                out=swap_diag[:, h, :], in0=pair_swap[:], scalar1=bias[:, h : h + 1], scalar2=0.0, op0=MULT, op1=ADD
-            )
+
+        turn_quarter(0)
+        turn_quarter(1)
+        quantise_quarter(0)
+        quantise_quarter(1)
+
+        tables_ps = psum_rot.tile([P, 2 * S], BF16, tag="rot")
+        for j in range(TOKEN_TILES):
+            nc.tensor.transpose(tables_ps[:, j * P : (j + 1) * P], cos_rows[:, j, :], ident_bf[:])
+        for j in range(TOKEN_TILES):
+            nc.tensor.transpose(tables_ps[:, S + j * P : S + (j + 1) * P], partner_rows[:, j, :], ident_bf[:])
+        tables_t = const.tile([P, 2 * S], BF16)
+        nc.scalar.copy(out=tables_t[:], in_=tables_ps[:])
+        cos_t = tables_t[:, 0:S]
+        partner_t = tables_t[:, S : 2 * S]
+
         roped_bias = const.tile([P, TOKEN_TILES, ROW_WIDTH], F32)
-        for j in range(TOKEN_TILES):
-            rb_ps = psum_acc.tile([P, S], F32, tag="acc")
+
+        def rope_bias(j):
+            rb_ps = psum_rot.tile([P, S], F32, tag="rot")
             tokens = slice(j * P, (j + 1) * P)
             nc.tensor.matmul(
                 out=rb_ps[:], lhsT=cos_t[:, tokens], rhs=own_diag[:].rearrange("p h d -> p (h d)"), start=True, stop=False
@@ -181,109 +212,138 @@ def tile_lineartransformerblock_pa_kernel(tc, x, cos, sin, Wq_words, Wq_scales, 
                 start=False,
                 stop=True,
             )
-            nc.vector.tensor_copy(out=roped_bias[:, j, :], in_=rb_ps[:])
+            nc.scalar.copy(out=roped_bias[:, j, :], in_=rb_ps[:])
 
-        for q in range(QUARTERS, QUARTERS_AHEAD):
-            transpose_quarter(q)
+        acc_of = {}
+        made_of = {}
 
-        def project_columns(b, h):
+        def multiply(unit):
+            kind, b, i = unit
             acc = psum_acc.tile([P, S], F32, tag="acc")
+            acc_of[unit] = acc
             for g in range(PASSES):
                 x_codes, x_planes = mx_of[(b, g)]
-                nc.tensor.matmul_mx(
-                    out=acc[:],
-                    lhsT=w_words[:, g, 2 * D * h : 2 * D * (h + 1)].bitcast(FP4X4),
-                    lhsT_scale=w_planes[:, g, D * h : D * (h + 1)],
-                    rhs=x_codes[:].bitcast(FP8X4),
-                    rhs_scale=x_planes[:],
-                    start=(g == 0),
-                    stop=(g == PASSES - 1),
-                )
-            own = prod_pool.tile([P, S], F32)
-            nc.vector.scalar_tensor_tensor(
-                out=own[:], in0=acc[:], scalar=bias[:, h : h + 1], in1=cos_t[:], op0=ADD, op1=MULT
-            )
-            other = prod_pool.tile([P, S], F32)
-            nc.vector.scalar_tensor_tensor(
-                out=other[:], in0=acc[:], scalar=bias[:, h : h + 1], in1=partner_t[:], op0=ADD, op1=MULT
-            )
-            return own, other
+                if kind == "col":
+                    nc.tensor.matmul_mx(
+                        out=acc[:],
+                        lhsT=w_words[:, g, 2 * D * i : 2 * D * (i + 1)].bitcast(FP4X4),
+                        lhsT_scale=w_planes[:, g, D * i : D * (i + 1)],
+                        rhs=x_codes[:].bitcast(FP8X4),
+                        rhs_scale=x_planes[:],
+                        start=(g == 0),
+                        stop=(g == PASSES - 1),
+                    )
+                else:
+                    tokens = slice(i * P, (i + 1) * P)
+                    nc.tensor.matmul_mx(
+                        out=acc[:],
+                        lhsT=x_codes[:, tokens].bitcast(FP8X4),
+                        lhsT_scale=x_planes[:, tokens],
+                        rhs=w_words[:, g, 0 : 2 * ROW_WIDTH].bitcast(FP4X4),
+                        rhs_scale=w_planes[:, g, 0:ROW_WIDTH],
+                        start=(g == 0),
+                        stop=(g == PASSES - 1),
+                    )
 
-        def rotate(b, h, own, other):
-            rot = psum_rot.tile([P, TOKEN_TILES, D], F32)
-            for j in range(TOKEN_TILES):
-                tokens = slice(j * P, (j + 1) * P)
-                nc.tensor.matmul(
-                    out=rot[:, j, :], lhsT=own[:, tokens], rhs=ident[:], is_transpose=True, start=True, stop=False
+        def products(unit):
+            kind, b, i = unit
+            acc = acc_of[unit]
+            if kind == "col":
+                own = prod_pool.tile([P, S], F32)
+                nc.vector.scalar_tensor_tensor(
+                    out=own[:], in0=acc[:], scalar=bias[:, i : i + 1], in1=cos_t, op0=ADD, op1=MULT
                 )
-                nc.tensor.matmul(
-                    out=rot[:, j, :], lhsT=other[:, tokens], rhs=pair_swap[:], is_transpose=True, start=False, stop=True
+                other = prod_pool.tile([P, S], F32)
+                nc.vector.scalar_tensor_tensor(
+                    out=other[:], in0=acc[:], scalar=bias[:, i : i + 1], in1=partner_t, op0=ADD, op1=MULT
                 )
-            res = res_pool.tile([P, TOKEN_TILES * D], F32)
-            nc.scalar.activation(out=res[:], in_=rot[:].rearrange("p j d -> p (j d)"), func=RELU)
-            nc.sync.dma_start(out=out[b, h].rearrange("(p j) d -> p (j d)", j=TOKEN_TILES), in_=res[:])
-
-        def project_rows(b, j):
-            acc = psum_acc.tile([P, S], F32, tag="acc")
-            tokens = slice(j * P, (j + 1) * P)
-            for g in range(PASSES):
-                x_codes, x_planes = mx_of[(b, g)]
-                nc.tensor.matmul_mx(
-                    out=acc[:],
-                    lhsT=x_codes[:, tokens].bitcast(FP8X4),
-                    lhsT_scale=x_planes[:, tokens],
-                    rhs=w_words[:, g, 0 : 2 * ROW_WIDTH].bitcast(FP4X4),
-                    rhs_scale=w_planes[:, g, 0:ROW_WIDTH],
-                    start=(g == 0),
-                    stop=(g == PASSES - 1),
+                made_of[unit] = (own, other)
+            else:
+                straight = row_pool.tile([P, ROW_HEADS, D], F32)
+                nc.vector.tensor_tensor(
+                    out=straight[:],
+                    in0=acc[:].rearrange("p (h d) -> p h d", h=ROW_HEADS),
+                    in1=cos_rows[:, i, :].unsqueeze(1).to_broadcast([P, ROW_HEADS, D]),
+                    op=MULT,
                 )
-            straight = prod_pool.tile([P, ROW_HEADS, D], F32)
-            nc.vector.tensor_tensor(
-                out=straight[:],
-                in0=acc[:].rearrange("p (h d) -> p h d", h=ROW_HEADS),
-                in1=cos_rows[:, j, :].unsqueeze(1).to_broadcast([P, ROW_HEADS, D]),
-                op=MULT,
-            )
-            crossed = prod_pool.tile([P, ROW_HEADS, D // 2, 2], F32)
-            nc.vector.tensor_tensor(
-                out=crossed[:],
-                in0=acc[:].rearrange("p (h i e) -> p h i e", h=ROW_HEADS, e=2)[:, :, :, ::-1],
-                in1=signed_rows[:, j, :]
-                .rearrange("p (i e) -> p i e", e=2)
-                .unsqueeze(1)
-                .to_broadcast([P, ROW_HEADS, D // 2, 2]),
-                op=MULT,
-            )
-            biased = sum_pool.tile([P, ROW_WIDTH], F32)
-            nc.gpsimd.tensor_tensor(
-                out=biased[:], in0=straight[:].rearrange("p h d -> p (h d)"), in1=roped_bias[:, j, :], op=ADD
-            )
-            total = sum_pool.tile([P, ROW_WIDTH], F32)
-            nc.gpsimd.tensor_tensor(
-                out=total[:], in0=biased[:], in1=crossed[:].rearrange("p h i e -> p (h i e)"), op=ADD
-            )
-            return total
+                crossed = row_pool.tile([P, ROW_HEADS, D // 2, 2], F32)
+                nc.vector.tensor_tensor(
+                    out=crossed[:],
+                    in0=acc[:].rearrange("p (h i e) -> p h i e", h=ROW_HEADS, e=2)[:, :, :, ::-1],
+                    in1=signed_rows[:, i, :]
+                    .rearrange("p (i e) -> p i e", e=2)
+                    .unsqueeze(1)
+                    .to_broadcast([P, ROW_HEADS, D // 2, 2]),
+                    op=MULT,
+                )
+                partial = row_pool.tile([P, ROW_WIDTH], F32)
+                nc.gpsimd.tensor_tensor(
+                    out=partial[:],
+                    in0=straight[:].rearrange("p h d -> p (h d)"),
+                    in1=crossed[:].rearrange("p h i e -> p (h i e)"),
+                    op=ADD,
+                )
+                total = row_pool.tile([P, ROW_WIDTH], F32)
+                nc.gpsimd.tensor_tensor(out=total[:], in0=partial[:], in1=roped_bias[:, i, :], op=ADD)
+                made_of[unit] = total
 
-        def finish_rows(b, j, total):
-            res_rows = res_pool.tile([P, ROW_HEADS, D], F32)
-            nc.scalar.activation(out=res_rows[:].rearrange("p h d -> p (h d)"), in_=total[:], func=RELU)
-            nc.sync.dma_start(
-                out=out[b, 0:ROW_HEADS].rearrange("h (p j) d -> p j h d", j=TOKEN_TILES)[:, j], in_=res_rows[:]
-            )
+        def finish(unit):
+            kind, b, i = unit
+            if kind == "col":
+                own, other = made_of[unit]
+                rot = psum_rot.tile([P, TOKEN_TILES, D], F32, tag="rot")
+                for j in range(TOKEN_TILES):
+                    tokens = slice(j * P, (j + 1) * P)
+                    nc.tensor.matmul(
+                        out=rot[:, j, :], lhsT=own[:, tokens], rhs=ident[:], is_transpose=True, start=True, stop=False
+                    )
+                    nc.tensor.matmul(
+                        out=rot[:, j, :],
+                        lhsT=other[:, tokens],
+                        rhs=pair_swap[:],
+                        is_transpose=True,
+                        start=False,
+                        stop=True,
+                    )
+                res = res_pool.tile([P, TOKEN_TILES * D], F32)
+                nc.scalar.activation(out=res[:], in_=rot[:].rearrange("p j d -> p (j d)"), func=RELU)
+                nc.sync.dma_start(out=out[b, i].rearrange("(p j) d -> p (j d)", j=TOKEN_TILES), in_=res[:])
+            else:
+                res_rows = res_pool.tile([P, ROW_HEADS, D], F32)
+                nc.scalar.activation(out=res_rows[:].rearrange("p h d -> p (h d)"), in_=made_of[unit][:], func=RELU)
+                nc.sync.dma_start(
+                    out=out[b, 0:ROW_HEADS].rearrange("h (p j) d -> p j h d", j=TOKEN_TILES)[:, i], in_=res_rows[:]
+                )
 
-        products = {}
-        totals = {}
-        for slot in range(SLOTS + 2):
-            if slot + QUARTERS_AHEAD < B * QUARTERS:
-                sort_quarter(slot + QUARTERS_AHEAD)
-            if slot < SLOTS:
-                products[slot] = project_columns(slot // COL_HEADS, ROW_HEADS + slot % COL_HEADS)
-                totals[slot] = project_rows(slot // TOKEN_TILES, slot % TOKEN_TILES)
-            if 1 <= slot <= SLOTS:
-                before = slot - 1
-                rotate(before // COL_HEADS, ROW_HEADS + before % COL_HEADS, products[before][0], products[before][1])
-            if slot >= 2:
-                before = slot - 2
-                finish_rows(before // TOKEN_TILES, before % TOKEN_TILES, totals[before])
-            if slot + QUARTERS_AHEAD < B * QUARTERS:
-                transpose_quarter(slot + QUARTERS_AHEAD)
+        slots = unit_slots()
+        for slot in range(len(slots) + 1):
+            turning = quarters_of_slot(slot)
+            for q in turning:
+                if q >= UNSORTED:
+                    sort_quarter(q)
+            now = slots[slot] if slot < len(slots) else []
+            for unit in now:
+                multiply(unit)
+            if slot >= 1:
+                for unit in slots[slot - 1]:
+                    if unit[0] == "col":
+                        finish(unit)
+            for q in turning:
+                turn_quarter(q)
+            if slot < 2:
+                rope_bias(2 * slot)
+                rope_bias(2 * slot + 1)
+            if slot == 0:
+                products(now[0])
+                quantise_quarter(turning[0])
+                products(now[1])
+                quantise_quarter(turning[1])
+            else:
+                for unit in now:
+                    products(unit)
+                for q in turning:
+                    quantise_quarter(q)
+            if slot >= ROW_LAG:
+                for unit in slots[slot - ROW_LAG]:
+                    if unit[0] == "row":
+                        finish(unit)

@@ -23,32 +23,14 @@ PASSES = C // K_PASS
 TOKEN_TILES = S // P
 QUARTERS = 2 * PASSES
 HALF = S // 2
-ROW_HEADS = 4
-ROW_WIDTH = ROW_HEADS * D
-ROW_BATCHES = 3
-ROW_LAG = 4
 UNSORTED = QUARTERS
 
 FLOPS = 2 * B * S * C * E
 
 
-def unit_slots():
-    slots = [
-        [("row", 0, 0), ("row", 0, 1)],
-        [("col", 0, 4), ("row", 0, 2)],
-        [("col", 0, 5), ("row", 0, 3)],
-        [("col", 0, 6), ("col", 0, 7)],
-    ]
-    for b in range(1, B):
-        for i in range(4):
-            first = ("row", b, i) if b < ROW_BATCHES else ("col", b, i)
-            slots.append([("col", b, ROW_HEADS + i), first])
-    return slots
-
-
 def quarters_of_slot(slot):
-    if slot < 3:
-        return [2 * slot + 2, 2 * slot + 3]
+    if slot == 0:
+        return [QUARTERS, QUARTERS + 1]
     return [slot + 5] if slot + 5 < B * QUARTERS else []
 
 
@@ -62,7 +44,6 @@ def tile_lineartransformerblock_pa_kernel(tc, x, cos, sin, Wq_words, Wq_scales, 
         stage = ctx.enter_context(tc.tile_pool(name="stage", bufs=4))
         mx_pool = ctx.enter_context(tc.tile_pool(name="mx_pool", bufs=2 * PASSES))
         prod_pool = ctx.enter_context(tc.tile_pool(name="prod_pool", bufs=4))
-        row_pool = ctx.enter_context(tc.tile_pool(name="row_pool", bufs=6))
         res_pool = ctx.enter_context(tc.tile_pool(name="res_pool", bufs=4))
         psum_x = ctx.enter_context(tc.psum_pool(name="psum_x", bufs=2))
         psum_acc = ctx.enter_context(tc.psum_pool(name="psum_acc", bufs=4))
@@ -89,19 +70,17 @@ def tile_lineartransformerblock_pa_kernel(tc, x, cos, sin, Wq_words, Wq_scales, 
         w_words = const.tile([P, PASSES, 2 * E], U8, align_bytes=64)
         w_words_i32 = w_words[:].bitcast(I32)
         w_source_i32 = Wq_words.bitcast(I32).rearrange("g p n -> p g n")
-        row_words = ROW_WIDTH // 2
+        row_words = E // 4
         scale_words = Wq_scales.bitcast(I32)
 
-        load_quarter(0)
-        load_quarter(1)
+        for q in range(QUARTERS):
+            load_quarter(q)
         for quadrant in range(4):
             nc.sync.dma_start(
                 out=w_planes[32 * quadrant : 32 * quadrant + 4].bitcast(I32),
                 in_=scale_words[:, 4 * quadrant : 4 * quadrant + 4, :].rearrange("g r n -> r g n"),
             )
         nc.sync.dma_start(out=w_words_i32[:, :, 0:row_words], in_=w_source_i32[:, :, 0:row_words])
-        load_quarter(2)
-        load_quarter(3)
         nc.sync.dma_start(out=w_words_i32[:, :, row_words:], in_=w_source_i32[:, :, row_words:])
         for q in range(QUARTERS, B * QUARTERS):
             load_quarter(q)
@@ -127,24 +106,11 @@ def tile_lineartransformerblock_pa_kernel(tc, x, cos, sin, Wq_words, Wq_scales, 
         partner_pairs = partner_rows[:].rearrange("p j (i e) -> p (j i) e", e=2)
         nc.vector.tensor_copy(out=partner_pairs[:, :, 0:1], in_=sin_pairs[:, :, 1:2])
         nc.vector.tensor_scalar_mul(out=partner_pairs[:, :, 1:2], in0=sin_pairs[:, :, 0:1], scalar1=-1.0)
-        signed_rows = const.tile([P, TOKEN_TILES, D], BF16)
-        signed_pairs = signed_rows[:].rearrange("p j (i e) -> p (j i) e", e=2)
-        nc.gpsimd.tensor_scalar(
-            out=signed_pairs[:, :, 0:1], in0=sin_pairs[:, :, 0:1], scalar1=-1.0, scalar2=0.0, op0=MULT, op1=ADD
-        )
-        nc.gpsimd.tensor_scalar(
-            out=signed_pairs[:, :, 1:2], in0=sin_pairs[:, :, 1:2], scalar1=1.0, scalar2=0.0, op0=MULT, op1=ADD
-        )
 
         bias = const.tile([P, H], F32)
         bias_ps = psum_rot.tile([P, 2 * S], BF16, tag="rot")
         nc.tensor.transpose(bias_ps[:, 0:P], bq_rows[:], ident_bf[:])
         nc.scalar.copy(out=bias[:], in_=bias_ps[:, 0:H])
-        own_diag = const.tile([P, ROW_HEADS, D], BF16)
-        swap_diag = const.tile([P, ROW_HEADS, D], BF16)
-        for h in range(ROW_HEADS):
-            nc.vector.tensor_scalar_mul(out=own_diag[:, h, :], in0=ident[:], scalar1=bias[:, h : h + 1])
-            nc.vector.tensor_scalar_mul(out=swap_diag[:, h, :], in0=pair_swap[:], scalar1=bias[:, h : h + 1])
 
         sorted_of = {}
         grouped_of = {}
@@ -182,10 +148,9 @@ def tile_lineartransformerblock_pa_kernel(tc, x, cos, sin, Wq_words, Wq_scales, 
                 out=x_codes[:, tokens].bitcast(FP8X4), scales=x_planes[:, tokens], in_=grouped_of[q][:]
             )
 
-        turn_quarter(0)
-        turn_quarter(1)
-        quantise_quarter(0)
-        quantise_quarter(1)
+        for q in range(QUARTERS):
+            turn_quarter(q)
+            quantise_quarter(q)
 
         tables_ps = psum_rot.tile([P, 2 * S], BF16, tag="rot")
         for j in range(TOKEN_TILES):
@@ -197,153 +162,66 @@ def tile_lineartransformerblock_pa_kernel(tc, x, cos, sin, Wq_words, Wq_scales, 
         cos_t = tables_t[:, 0:S]
         partner_t = tables_t[:, S : 2 * S]
 
-        roped_bias = const.tile([P, TOKEN_TILES, ROW_WIDTH], F32)
-
-        def rope_bias(j):
-            rb_ps = psum_rot.tile([P, S], F32, tag="rot")
-            tokens = slice(j * P, (j + 1) * P)
-            nc.tensor.matmul(
-                out=rb_ps[:], lhsT=cos_t[:, tokens], rhs=own_diag[:].rearrange("p h d -> p (h d)"), start=True, stop=False
-            )
-            nc.tensor.matmul(
-                out=rb_ps[:],
-                lhsT=partner_t[:, tokens],
-                rhs=swap_diag[:].rearrange("p h d -> p (h d)"),
-                start=False,
-                stop=True,
-            )
-            nc.scalar.copy(out=roped_bias[:, j, :], in_=rb_ps[:])
-
         acc_of = {}
         made_of = {}
 
         def multiply(unit):
-            kind, b, i = unit
+            b, h = unit
             acc = psum_acc.tile([P, S], F32, tag="acc")
             acc_of[unit] = acc
             for g in range(PASSES):
                 x_codes, x_planes = mx_of[(b, g)]
-                if kind == "col":
-                    nc.tensor.matmul_mx(
-                        out=acc[:],
-                        lhsT=w_words[:, g, 2 * D * i : 2 * D * (i + 1)].bitcast(FP4X4),
-                        lhsT_scale=w_planes[:, g, D * i : D * (i + 1)],
-                        rhs=x_codes[:].bitcast(FP8X4),
-                        rhs_scale=x_planes[:],
-                        start=(g == 0),
-                        stop=(g == PASSES - 1),
-                    )
-                else:
-                    tokens = slice(i * P, (i + 1) * P)
-                    nc.tensor.matmul_mx(
-                        out=acc[:],
-                        lhsT=x_codes[:, tokens].bitcast(FP8X4),
-                        lhsT_scale=x_planes[:, tokens],
-                        rhs=w_words[:, g, 0 : 2 * ROW_WIDTH].bitcast(FP4X4),
-                        rhs_scale=w_planes[:, g, 0:ROW_WIDTH],
-                        start=(g == 0),
-                        stop=(g == PASSES - 1),
-                    )
+                nc.tensor.matmul_mx(
+                    out=acc[:],
+                    lhsT=w_words[:, g, 2 * D * h : 2 * D * (h + 1)].bitcast(FP4X4),
+                    lhsT_scale=w_planes[:, g, D * h : D * (h + 1)],
+                    rhs=x_codes[:].bitcast(FP8X4),
+                    rhs_scale=x_planes[:],
+                    start=(g == 0),
+                    stop=(g == PASSES - 1),
+                )
 
         def products(unit):
-            kind, b, i = unit
+            b, h = unit
             acc = acc_of[unit]
-            if kind == "col":
-                own = prod_pool.tile([P, S], F32)
-                nc.vector.scalar_tensor_tensor(
-                    out=own[:], in0=acc[:], scalar=bias[:, i : i + 1], in1=cos_t, op0=ADD, op1=MULT
-                )
-                other = prod_pool.tile([P, S], F32)
-                nc.vector.scalar_tensor_tensor(
-                    out=other[:], in0=acc[:], scalar=bias[:, i : i + 1], in1=partner_t, op0=ADD, op1=MULT
-                )
-                made_of[unit] = (own, other)
-            else:
-                straight = row_pool.tile([P, ROW_HEADS, D], F32)
-                nc.vector.tensor_tensor(
-                    out=straight[:],
-                    in0=acc[:].rearrange("p (h d) -> p h d", h=ROW_HEADS),
-                    in1=cos_rows[:, i, :].unsqueeze(1).to_broadcast([P, ROW_HEADS, D]),
-                    op=MULT,
-                )
-                crossed = row_pool.tile([P, ROW_HEADS, D // 2, 2], F32)
-                nc.vector.tensor_tensor(
-                    out=crossed[:],
-                    in0=acc[:].rearrange("p (h i e) -> p h i e", h=ROW_HEADS, e=2)[:, :, :, ::-1],
-                    in1=signed_rows[:, i, :]
-                    .rearrange("p (i e) -> p i e", e=2)
-                    .unsqueeze(1)
-                    .to_broadcast([P, ROW_HEADS, D // 2, 2]),
-                    op=MULT,
-                )
-                partial = row_pool.tile([P, ROW_WIDTH], F32)
-                nc.gpsimd.tensor_tensor(
-                    out=partial[:],
-                    in0=straight[:].rearrange("p h d -> p (h d)"),
-                    in1=crossed[:].rearrange("p h i e -> p (h i e)"),
-                    op=ADD,
-                )
-                total = row_pool.tile([P, ROW_WIDTH], F32)
-                nc.gpsimd.tensor_tensor(out=total[:], in0=partial[:], in1=roped_bias[:, i, :], op=ADD)
-                made_of[unit] = total
+            own = prod_pool.tile([P, S], F32)
+            nc.vector.scalar_tensor_tensor(
+                out=own[:], in0=acc[:], scalar=bias[:, h : h + 1], in1=cos_t, op0=ADD, op1=MULT
+            )
+            other = prod_pool.tile([P, S], F32)
+            nc.vector.scalar_tensor_tensor(
+                out=other[:], in0=acc[:], scalar=bias[:, h : h + 1], in1=partner_t, op0=ADD, op1=MULT
+            )
+            made_of[unit] = (own, other)
 
         def finish(unit):
-            kind, b, i = unit
-            if kind == "col":
-                own, other = made_of[unit]
-                rot = psum_rot.tile([P, TOKEN_TILES, D], F32, tag="rot")
-                for j in range(TOKEN_TILES):
-                    tokens = slice(j * P, (j + 1) * P)
-                    nc.tensor.matmul(
-                        out=rot[:, j, :], lhsT=own[:, tokens], rhs=ident[:], is_transpose=True, start=True, stop=False
-                    )
-                    nc.tensor.matmul(
-                        out=rot[:, j, :],
-                        lhsT=other[:, tokens],
-                        rhs=pair_swap[:],
-                        is_transpose=True,
-                        start=False,
-                        stop=True,
-                    )
-                res = res_pool.tile([P, TOKEN_TILES * D], F32)
-                nc.scalar.activation(out=res[:], in_=rot[:].rearrange("p j d -> p (j d)"), func=RELU)
-                nc.sync.dma_start(out=out[b, i].rearrange("(p j) d -> p (j d)", j=TOKEN_TILES), in_=res[:])
-            else:
-                res_rows = res_pool.tile([P, ROW_HEADS, D], F32)
-                nc.scalar.activation(out=res_rows[:].rearrange("p h d -> p (h d)"), in_=made_of[unit][:], func=RELU)
-                nc.sync.dma_start(
-                    out=out[b, 0:ROW_HEADS].rearrange("h (p j) d -> p j h d", j=TOKEN_TILES)[:, i], in_=res_rows[:]
+            b, h = unit
+            own, other = made_of[unit]
+            rot = psum_rot.tile([P, TOKEN_TILES, D], F32, tag="rot")
+            for j in range(TOKEN_TILES):
+                tokens = slice(j * P, (j + 1) * P)
+                nc.tensor.matmul(
+                    out=rot[:, j, :], lhsT=own[:, tokens], rhs=ident[:], is_transpose=True, start=True, stop=False
                 )
+                nc.tensor.matmul(
+                    out=rot[:, j, :], lhsT=other[:, tokens], rhs=pair_swap[:], is_transpose=True, start=False, stop=True
+                )
+            res = res_pool.tile([P, TOKEN_TILES * D], F32)
+            nc.scalar.activation(out=res[:], in_=rot[:].rearrange("p j d -> p (j d)"), func=RELU)
+            nc.sync.dma_start(out=out[b, h].rearrange("(p j) d -> p (j d)", j=TOKEN_TILES), in_=res[:])
 
-        slots = unit_slots()
+        slots = [[(n // H, n % H), ((n + 1) // H, (n + 1) % H)] for n in range(0, B * H, 2)]
         for slot in range(len(slots) + 1):
             turning = quarters_of_slot(slot)
             for q in turning:
-                if q >= UNSORTED:
-                    sort_quarter(q)
+                sort_quarter(q)
             now = slots[slot] if slot < len(slots) else []
             for unit in now:
                 multiply(unit)
+                products(unit)
             if slot >= 1:
                 for unit in slots[slot - 1]:
-                    if unit[0] == "col":
-                        finish(unit)
+                    finish(unit)
             for q in turning:
                 turn_quarter(q)
-            if slot < 2:
-                rope_bias(2 * slot)
-                rope_bias(2 * slot + 1)
-            if slot == 0:
-                products(now[0])
-                quantise_quarter(turning[0])
-                products(now[1])
-                quantise_quarter(turning[1])
-            else:
-                for unit in now:
-                    products(unit)
-                for q in turning:
-                    quantise_quarter(q)
-            if slot >= ROW_LAG:
-                for unit in slots[slot - ROW_LAG]:
-                    if unit[0] == "row":
-                        finish(unit)
+                quantise_quarter(q)

@@ -28,10 +28,14 @@ UNSORTED = QUARTERS
 FLOPS = 2 * B * S * C * E
 
 
-def quarters_of_slot(slot):
-    if slot == 0:
-        return [QUARTERS, QUARTERS + 1]
-    return [slot + 5] if slot + 5 < B * QUARTERS else []
+GROUP = 4
+ROUNDS = B * H // GROUP
+
+
+def quarters_of_round(n):
+    if n == 0:
+        return list(range(QUARTERS, 2 * QUARTERS))
+    return [q for q in (2 * n + 6, 2 * n + 7) if q < B * QUARTERS]
 
 
 def tile_lineartransformerblock_pa_kernel(tc, x, cos, sin, Wq_words, Wq_scales, bq, out):
@@ -40,10 +44,10 @@ def tile_lineartransformerblock_pa_kernel(tc, x, cos, sin, Wq_words, Wq_scales, 
         ctx.enter_context(tc.manual_schedule())
         const = ctx.enter_context(tc.tile_pool(name="const", bufs=1))
         x_pool = ctx.enter_context(tc.tile_pool(name="x_pool", bufs=B * QUARTERS))
-        sort_pool = ctx.enter_context(tc.tile_pool(name="sort_pool", bufs=3))
+        sort_pool = ctx.enter_context(tc.tile_pool(name="sort_pool", bufs=QUARTERS))
         stage = ctx.enter_context(tc.tile_pool(name="stage", bufs=4))
         mx_pool = ctx.enter_context(tc.tile_pool(name="mx_pool", bufs=2 * PASSES))
-        prod_pool = ctx.enter_context(tc.tile_pool(name="prod_pool", bufs=4))
+        prod_pool = ctx.enter_context(tc.tile_pool(name="prod_pool", bufs=2 * GROUP))
         res_pool = ctx.enter_context(tc.tile_pool(name="res_pool", bufs=4))
         psum_x = ctx.enter_context(tc.psum_pool(name="psum_x", bufs=2))
         psum_acc = ctx.enter_context(tc.psum_pool(name="psum_acc", bufs=4))
@@ -210,18 +214,17 @@ def tile_lineartransformerblock_pa_kernel(tc, x, cos, sin, Wq_words, Wq_scales, 
             nc.scalar.activation(out=res[:], in_=rot[:].rearrange("p j d -> p (j d)"), func=RELU)
             nc.sync.dma_start(out=out[b, h].rearrange("(p j) d -> p (j d)", j=TOKEN_TILES), in_=res[:])
 
-        slots = [[(n // H, n % H), ((n + 1) // H, (n + 1) % H)] for n in range(0, B * H, 2)]
-        for slot in range(len(slots) + 1):
-            turning = quarters_of_slot(slot)
+        for n in range(ROUNDS + 1):
+            turning = quarters_of_round(n)
             for q in turning:
                 sort_quarter(q)
-            now = slots[slot] if slot < len(slots) else []
-            for unit in now:
-                multiply(unit)
-                products(unit)
-            if slot >= 1:
-                for unit in slots[slot - 1]:
-                    finish(unit)
+            if n < ROUNDS:
+                for unit in range(GROUP * n, GROUP * (n + 1)):
+                    multiply((unit // H, unit % H))
+                    products((unit // H, unit % H))
+            if n >= 1:
+                for unit in range(GROUP * (n - 1), GROUP * n):
+                    finish((unit // H, unit % H))
             for q in turning:
                 turn_quarter(q)
                 quantise_quarter(q)

@@ -49,9 +49,8 @@ def tile_lineartransformerblock_pa_kernel(tc, x, cos, sin, Wq_words, Wq_scales, 
         mx_pool = ctx.enter_context(tc.tile_pool(name="mx_pool", bufs=2 * PASSES))
         prod_pool = ctx.enter_context(tc.tile_pool(name="prod_pool", bufs=2 * GROUP))
         res_pool = ctx.enter_context(tc.tile_pool(name="res_pool", bufs=4))
-        psum_x = ctx.enter_context(tc.psum_pool(name="psum_x", bufs=2))
         psum_acc = ctx.enter_context(tc.psum_pool(name="psum_acc", bufs=4))
-        psum_rot = ctx.enter_context(tc.psum_pool(name="psum_rot", bufs=2))
+        psum_rot = ctx.enter_context(tc.psum_pool(name="psum_rot", bufs=4))
 
         w_planes = const.tile([P, PASSES, E], U8, align_bytes=64)
         nc.vector.memset(w_planes[:].bitcast(I32), 0)
@@ -130,7 +129,7 @@ def tile_lineartransformerblock_pa_kernel(tc, x, cos, sin, Wq_words, Wq_scales, 
                 words = x_quarters[q][:].bitcast(F32).rearrange("p j (q u) -> p j u q", u=2)
             else:
                 words = sorted_of[q]
-            xt = psum_x.tile([P, 2, 2 * P], F32)
+            xt = psum_rot.tile([P, 2, 2 * P], F32, tag="rot")
             for u in range(2):
                 for jj in range(2):
                     nc.tensor.transpose(xt[:, u, jj * P : (jj + 1) * P], words[:, jj, u, :], ident[:])

@@ -30,6 +30,7 @@ FLOPS = 2 * B * S * C * E
 
 GROUP = 4
 ROUNDS = B * H // GROUP
+ROW_HEADS = [0, GROUP]
 
 
 def quarters_of_round(n):
@@ -43,32 +44,32 @@ def tile_lineartransformerblock_pa_kernel(tc, x, cos, sin, Wq_words, Wq_scales, 
     with ExitStack() as ctx:
         ctx.enter_context(tc.manual_schedule())
         const = ctx.enter_context(tc.tile_pool(name="const", bufs=1))
-        x_pool = ctx.enter_context(tc.tile_pool(name="x_pool", bufs=B * QUARTERS))
+        x_pool = ctx.enter_context(tc.tile_pool(name="x_pool", bufs=B * PASSES))
         sort_pool = ctx.enter_context(tc.tile_pool(name="sort_pool", bufs=QUARTERS))
         stage = ctx.enter_context(tc.tile_pool(name="stage", bufs=4))
         mx_pool = ctx.enter_context(tc.tile_pool(name="mx_pool", bufs=2 * PASSES))
         prod_pool = ctx.enter_context(tc.tile_pool(name="prod_pool", bufs=2 * GROUP))
+        row_pool = ctx.enter_context(tc.tile_pool(name="row_pool", bufs=2))
         res_pool = ctx.enter_context(tc.tile_pool(name="res_pool", bufs=4))
         psum_acc = ctx.enter_context(tc.psum_pool(name="psum_acc", bufs=4))
         psum_rot = ctx.enter_context(tc.psum_pool(name="psum_rot", bufs=4))
 
-        w_planes = const.tile([P, PASSES, E], U8, align_bytes=64)
-        nc.vector.memset(w_planes[:].bitcast(I32), 0)
         bq_rows = const.tile([P, P], BF16)
         nc.vector.memset(bq_rows[:], 0.0)
+        nc.scalar.dma_start(out=bq_rows[0:H, :], in_=bq.rearrange("(h d) -> h d", d=D))
+        w_planes = const.tile([P, PASSES, E], U8, align_bytes=64)
+        nc.vector.memset(w_planes[:].bitcast(I32), 0)
 
-        x_quarters = []
+        x_tiles = {}
 
-        def load_quarter(q):
-            b, half, g = q // QUARTERS, (q % QUARTERS) // 2, q % 2
-            x_sb = x_pool.tile([P, 2, K_PASS], BF16)
+        def load_x(b, g, rows):
+            if (b, g) not in x_tiles:
+                x_sb = x_pool.tile([P, TOKEN_TILES, K_PASS], BF16)
+                x_tiles[(b, g)] = x_sb
             nc.sync.dma_start(
-                out=x_sb[:],
-                in_=x[b].rearrange("(p j) c -> p j c", j=TOKEN_TILES)[
-                    :, 2 * half : 2 * half + 2, K_PASS * g : K_PASS * (g + 1)
-                ],
+                out=x_tiles[(b, g)][:, rows, :],
+                in_=x[b].rearrange("(p j) c -> p j c", j=TOKEN_TILES)[:, rows, K_PASS * g : K_PASS * (g + 1)],
             )
-            x_quarters.append(x_sb)
 
         w_words = const.tile([P, PASSES, 2 * E], U8, align_bytes=64)
         w_words_i32 = w_words[:].bitcast(I32)
@@ -76,23 +77,23 @@ def tile_lineartransformerblock_pa_kernel(tc, x, cos, sin, Wq_words, Wq_scales, 
         row_words = E // 4
         scale_words = Wq_scales.bitcast(I32)
 
-        for q in range(QUARTERS):
-            load_quarter(q)
+        cos_rows = const.tile([P, TOKEN_TILES, D], BF16)
+        nc.sync.dma_start(out=cos_rows[:], in_=cos.rearrange("(p j) d -> p j d", j=TOKEN_TILES))
+        sin_rows = const.tile([P, TOKEN_TILES, D], BF16)
+        nc.sync.dma_start(out=sin_rows[:], in_=sin.rearrange("(p j) d -> p j d", j=TOKEN_TILES))
+        load_x(0, 0, slice(0, 2))
+        load_x(0, 0, slice(2, 4))
+        load_x(0, 1, slice(0, 4))
+        nc.sync.dma_start(out=w_words_i32[:, :, 0:row_words], in_=w_source_i32[:, :, 0:row_words])
         for quadrant in range(4):
             nc.sync.dma_start(
                 out=w_planes[32 * quadrant : 32 * quadrant + 4].bitcast(I32),
                 in_=scale_words[:, 4 * quadrant : 4 * quadrant + 4, :].rearrange("g r n -> r g n"),
             )
-        nc.sync.dma_start(out=w_words_i32[:, :, 0:row_words], in_=w_source_i32[:, :, 0:row_words])
         nc.sync.dma_start(out=w_words_i32[:, :, row_words:], in_=w_source_i32[:, :, row_words:])
-        for q in range(QUARTERS, B * QUARTERS):
-            load_quarter(q)
-
-        nc.scalar.dma_start(out=bq_rows[0:H, :], in_=bq.rearrange("(h d) -> h d", d=D))
-        sin_rows = const.tile([P, TOKEN_TILES, D], BF16)
-        nc.scalar.dma_start(out=sin_rows[:], in_=sin.rearrange("(p j) d -> p j d", j=TOKEN_TILES))
-        cos_rows = const.tile([P, TOKEN_TILES, D], BF16)
-        nc.scalar.dma_start(out=cos_rows[:], in_=cos.rearrange("(p j) d -> p j d", j=TOKEN_TILES))
+        for b in range(1, B):
+            for g in range(PASSES):
+                load_x(b, g, slice(0, 4))
 
         ident = const.tile([P, P], F32)
         make_identity(nc, ident[:])
@@ -104,29 +105,23 @@ def tile_lineartransformerblock_pa_kernel(tc, x, cos, sin, Wq_words, Wq_scales, 
         nc.vector.tensor_copy(out=swap_pairs[:, :, 0:1], in_=ident_pairs[:, :, 1:2])
         nc.vector.tensor_copy(out=swap_pairs[:, :, 1:2], in_=ident_pairs[:, :, 0:1])
 
-        sin_pairs = sin_rows[:].rearrange("p j (i e) -> p (j i) e", e=2)
-        partner_rows = const.tile([P, TOKEN_TILES, D], BF16)
-        partner_pairs = partner_rows[:].rearrange("p j (i e) -> p (j i) e", e=2)
-        nc.vector.tensor_copy(out=partner_pairs[:, :, 0:1], in_=sin_pairs[:, :, 1:2])
-        nc.vector.tensor_scalar_mul(out=partner_pairs[:, :, 1:2], in0=sin_pairs[:, :, 0:1], scalar1=-1.0)
-
-        bias = const.tile([P, H], F32)
-        bias_ps = psum_rot.tile([P, 2 * S], BF16, tag="rot")
-        nc.tensor.transpose(bias_ps[:, 0:P], bq_rows[:], ident_bf[:])
-        nc.scalar.copy(out=bias[:], in_=bias_ps[:, 0:H])
-
         sorted_of = {}
         grouped_of = {}
         mx_of = {}
 
+        def quarter_words(q):
+            b, g, half = q // QUARTERS, (q % QUARTERS) // 2, q % 2
+            rows = x_tiles[(b, g)][:, 2 * half : 2 * half + 2, :]
+            return rows.bitcast(F32).rearrange("p j (q u) -> p j u q", u=2)
+
         def sort_quarter(q):
             x_sorted = sort_pool.tile([P, 2, 2, P], F32)
-            nc.scalar.copy(out=x_sorted[:], in_=x_quarters[q][:].bitcast(F32).rearrange("p j (q u) -> p j u q", u=2))
+            nc.scalar.copy(out=x_sorted[:], in_=quarter_words(q))
             sorted_of[q] = x_sorted[:]
 
         def turn_quarter(q):
             if q < UNSORTED:
-                words = x_quarters[q][:].bitcast(F32).rearrange("p j (q u) -> p j u q", u=2)
+                words = quarter_words(q)
             else:
                 words = sorted_of[q]
             xt = psum_rot.tile([P, 2, 2 * P], F32, tag="rot")
@@ -140,7 +135,7 @@ def tile_lineartransformerblock_pa_kernel(tc, x, cos, sin, Wq_words, Wq_scales, 
             grouped_of[q] = grouped
 
         def quantise_quarter(q):
-            b, half, g = q // QUARTERS, (q % QUARTERS) // 2, q % 2
+            b, g, half = q // QUARTERS, (q % QUARTERS) // 2, q % 2
             if half == 0:
                 x_codes = mx_pool.tile([P, S], U32, align_bytes=64)
                 x_planes = mx_pool.tile([P, S], U8, align_bytes=64)
@@ -151,38 +146,132 @@ def tile_lineartransformerblock_pa_kernel(tc, x, cos, sin, Wq_words, Wq_scales, 
                 out=x_codes[:, tokens].bitcast(FP8X4), scales=x_planes[:, tokens], in_=grouped_of[q][:]
             )
 
-        for q in range(QUARTERS):
+        partner_rows = const.tile([P, TOKEN_TILES, D], BF16)
+        sin_pairs = sin_rows[:].rearrange("p j (i e) -> p (j i) e", e=2)
+        partner_pairs = partner_rows[:].rearrange("p j (i e) -> p (j i) e", e=2)
+        nc.vector.tensor_copy(out=partner_pairs[:, :, 0:1], in_=sin_pairs[:, :, 1:2])
+        nc.vector.tensor_scalar_mul(out=partner_pairs[:, :, 1:2], in0=sin_pairs[:, :, 0:1], scalar1=-1.0)
+
+        def turn_table(rows):
+            table_ps = psum_rot.tile([P, S], BF16, tag="rot")
+            for j in range(TOKEN_TILES):
+                nc.tensor.transpose(table_ps[:, j * P : (j + 1) * P], rows[:, j, :], ident_bf[:])
+            return table_ps
+
+        cos_tile = const.tile([P, S], BF16)
+        cos_ps = turn_table(cos_rows)
+        nc.scalar.copy(out=cos_tile[:], in_=cos_ps[:])
+        turn_quarter(0)
+        partner_tile = const.tile([P, S], BF16)
+        partner_ps = turn_table(partner_rows)
+        nc.vector.tensor_copy(out=partner_tile[:], in_=partner_ps[:])
+        cos_t = cos_tile[:]
+        partner_t = partner_tile[:]
+
+        bias_ps = psum_rot.tile([P, len(ROW_HEADS) * D + H], F32, tag="rot")
+        for i, h in enumerate(ROW_HEADS):
+            nc.tensor.matmul(
+                out=bias_ps[:, i * D : (i + 1) * D],
+                lhsT=ident_bf[:, h : h + 1].to_broadcast([P, P]),
+                rhs=bq_rows[:],
+                start=True,
+                stop=True,
+            )
+        nc.tensor.matmul(
+            out=bias_ps[:, len(ROW_HEADS) * D :], lhsT=bq_rows[:], rhs=ident_bf[:, 0:H], start=True, stop=True
+        )
+        bias_sb = const.tile([P, len(ROW_HEADS) * D + H], F32)
+        nc.vector.tensor_copy(out=bias_sb[:], in_=bias_ps[:])
+        bias = bias_sb[:, len(ROW_HEADS) * D :]
+        quantise_quarter(0)
+
+        def swapped(tile):
+            return tile[:].rearrange("p (i e) -> p i e", e=2)[:, :, ::-1]
+
+        def pairs(tile):
+            return tile[:].rearrange("p (i e) -> p i e", e=2)
+
+        roped_bias = {}
+        for i, h in enumerate(ROW_HEADS):
+            spread = bias_sb[:, i * D : (i + 1) * D].unsqueeze(1).to_broadcast([P, TOKEN_TILES, D])
+            direct = row_pool.tile([P, TOKEN_TILES * D], F32)
+            nc.gpsimd.tensor_tensor(
+                out=direct[:].rearrange("p (j d) -> p j d", d=D), in0=spread, in1=cos_rows[:], op=MULT
+            )
+            crossed = row_pool.tile([P, TOKEN_TILES * D], F32)
+            nc.gpsimd.tensor_tensor(
+                out=crossed[:].rearrange("p (j d) -> p j d", d=D), in0=spread, in1=partner_rows[:], op=MULT
+            )
+            total = const.tile([P, TOKEN_TILES * D], F32, name="roped_bias%d" % i)
+            nc.gpsimd.tensor_tensor(out=pairs(total), in0=pairs(direct), in1=swapped(crossed), op=ADD)
+            roped_bias[h] = total
+        for q in range(1, QUARTERS):
             turn_quarter(q)
             quantise_quarter(q)
-
-        tables_ps = psum_rot.tile([P, 2 * S], BF16, tag="rot")
-        for j in range(TOKEN_TILES):
-            nc.tensor.transpose(tables_ps[:, j * P : (j + 1) * P], cos_rows[:, j, :], ident_bf[:])
-        for j in range(TOKEN_TILES):
-            nc.tensor.transpose(tables_ps[:, S + j * P : S + (j + 1) * P], partner_rows[:, j, :], ident_bf[:])
-        tables_t = const.tile([P, 2 * S], BF16)
-        nc.scalar.copy(out=tables_t[:], in_=tables_ps[:])
-        cos_t = tables_t[:, 0:S]
-        partner_t = tables_t[:, S : 2 * S]
 
         acc_of = {}
         made_of = {}
 
-        def multiply(unit):
+        def open_banks(n):
+            for unit in round_units(n):
+                acc = psum_acc.tile([P, S], F32, tag="acc")
+                acc_of[unit] = acc
+
+        def multiply_rows(unit):
             b, h = unit
-            acc = psum_acc.tile([P, S], F32, tag="acc")
-            acc_of[unit] = acc
-            for g in range(PASSES):
-                x_codes, x_planes = mx_of[(b, g)]
-                nc.tensor.matmul_mx(
-                    out=acc[:],
-                    lhsT=w_words[:, g, 2 * D * h : 2 * D * (h + 1)].bitcast(FP4X4),
-                    lhsT_scale=w_planes[:, g, D * h : D * (h + 1)],
-                    rhs=x_codes[:].bitcast(FP8X4),
-                    rhs_scale=x_planes[:],
-                    start=(g == 0),
-                    stop=(g == PASSES - 1),
-                )
+            for j in range(TOKEN_TILES):
+                columns = slice(j * P, (j + 1) * P)
+                for g in range(PASSES):
+                    x_codes, x_planes = mx_of[(b, g)]
+                    nc.tensor.matmul_mx(
+                        out=acc_of[unit][:, columns],
+                        lhsT=x_codes[:, columns].bitcast(FP8X4),
+                        lhsT_scale=x_planes[:, columns],
+                        rhs=w_words[:, g, 2 * D * h : 2 * D * (h + 1)].bitcast(FP4X4),
+                        rhs_scale=w_planes[:, g, D * h : D * (h + 1)],
+                        start=(g == 0),
+                        stop=(g == PASSES - 1),
+                    )
+
+        def row_products(unit):
+            acc = acc_of[unit]
+            row_own = row_pool.tile([P, TOKEN_TILES * D], F32)
+            nc.vector.tensor_tensor(out=row_own[:], in0=acc[:], in1=cos_rows[:].rearrange("p j d -> p (j d)"), op=MULT)
+            row_other = row_pool.tile([P, TOKEN_TILES * D], F32)
+            nc.vector.tensor_tensor(
+                out=row_other[:], in0=acc[:], in1=partner_rows[:].rearrange("p j d -> p (j d)"), op=MULT
+            )
+            row_part = row_pool.tile([P, TOKEN_TILES * D], F32)
+            nc.gpsimd.tensor_tensor(out=row_part[:], in0=row_own[:], in1=roped_bias[unit[1]][:], op=ADD)
+            row_sum = row_pool.tile([P, TOKEN_TILES * D], F32)
+            nc.gpsimd.tensor_tensor(out=pairs(row_sum), in0=pairs(row_part), in1=swapped(row_other), op=ADD)
+            made_of[unit] = row_sum
+
+        def finish_rows(unit):
+            b, h = unit
+            res = res_pool.tile([P, TOKEN_TILES * D], F32)
+            nc.scalar.activation(out=res[:], in_=made_of[unit][:], func=RELU)
+            nc.sync.dma_start(out=out[b, h].rearrange("(p j) d -> p (j d)", j=TOKEN_TILES), in_=res[:])
+
+        def multiply_pass(unit, g):
+            b, h = unit
+            x_codes, x_planes = mx_of[(b, g)]
+            nc.tensor.matmul_mx(
+                out=acc_of[unit][:],
+                lhsT=w_words[:, g, 2 * D * h : 2 * D * (h + 1)].bitcast(FP4X4),
+                lhsT_scale=w_planes[:, g, D * h : D * (h + 1)],
+                rhs=x_codes[:].bitcast(FP8X4),
+                rhs_scale=x_planes[:],
+                start=(g == 0),
+                stop=(g == PASSES - 1),
+            )
+
+        def round_units(n):
+            return [(unit // H, unit % H) for unit in range(GROUP * n, GROUP * (n + 1))]
+
+        open_banks(0)
+        for unit in round_units(0)[1:]:
+            multiply_pass(unit, 0)
 
         def products(unit):
             b, h = unit
@@ -218,12 +307,21 @@ def tile_lineartransformerblock_pa_kernel(tc, x, cos, sin, Wq_words, Wq_scales, 
             for q in turning:
                 sort_quarter(q)
             if n < ROUNDS:
-                for unit in range(GROUP * n, GROUP * (n + 1)):
-                    multiply((unit // H, unit % H))
-                    products((unit // H, unit % H))
+                if n > 0:
+                    open_banks(n)
+                row_unit = round_units(n)[0]
+                multiply_rows(row_unit)
+                row_products(row_unit)
+                for unit in round_units(n)[1:]:
+                    for g in range(PASSES):
+                        if n > 0 or g > 0:
+                            multiply_pass(unit, g)
+                    products(unit)
             if n >= 1:
-                for unit in range(GROUP * (n - 1), GROUP * n):
-                    finish((unit // H, unit % H))
+                for unit in round_units(n - 1)[1:]:
+                    finish(unit)
             for q in turning:
                 turn_quarter(q)
                 quantise_quarter(q)
+            if n < ROUNDS:
+                finish_rows(row_unit)

@@ -30,6 +30,7 @@ FLOPS = 2 * B * S * C * E
 
 GROUP = 4
 ROUNDS = B * H // GROUP
+WARM_BEFORE_X = 15
 ROW_HEADS = [0, GROUP]
 
 
@@ -50,13 +51,14 @@ def tile_lineartransformerblock_pa_kernel(tc, x, cos, sin, Wq_words, Wq_scales, 
         mx_pool = ctx.enter_context(tc.tile_pool(name="mx_pool", bufs=2 * PASSES))
         prod_pool = ctx.enter_context(tc.tile_pool(name="prod_pool", bufs=2 * GROUP))
         row_pool = ctx.enter_context(tc.tile_pool(name="row_pool", bufs=2))
-        res_pool = ctx.enter_context(tc.tile_pool(name="res_pool", bufs=4))
+        res_pool = ctx.enter_context(tc.tile_pool(name="res_pool", bufs=8))
         psum_acc = ctx.enter_context(tc.psum_pool(name="psum_acc", bufs=4))
         psum_rot = ctx.enter_context(tc.psum_pool(name="psum_rot", bufs=4))
 
+        zeros = const.tile([P, P], BF16)
+        nc.vector.memset(zeros[:], 0.0)
         bq_rows = const.tile([P, P], BF16)
         nc.vector.memset(bq_rows[:], 0.0)
-        nc.scalar.dma_start(out=bq_rows[0:H, :], in_=bq.rearrange("(h d) -> h d", d=D))
         w_planes = const.tile([P, PASSES, E], U8, align_bytes=64)
         nc.vector.memset(w_planes[:].bitcast(I32), 0)
 
@@ -77,10 +79,6 @@ def tile_lineartransformerblock_pa_kernel(tc, x, cos, sin, Wq_words, Wq_scales, 
         row_words = E // 4
         scale_words = Wq_scales.bitcast(I32)
 
-        cos_rows = const.tile([P, TOKEN_TILES, D], BF16)
-        nc.sync.dma_start(out=cos_rows[:], in_=cos.rearrange("(p j) d -> p j d", j=TOKEN_TILES))
-        sin_rows = const.tile([P, TOKEN_TILES, D], BF16)
-        nc.sync.dma_start(out=sin_rows[:], in_=sin.rearrange("(p j) d -> p j d", j=TOKEN_TILES))
         load_x(0, 0, slice(0, 2))
         load_x(0, 0, slice(2, 4))
         load_x(0, 1, slice(0, 4))
@@ -90,6 +88,8 @@ def tile_lineartransformerblock_pa_kernel(tc, x, cos, sin, Wq_words, Wq_scales, 
                 out=w_planes[32 * quadrant : 32 * quadrant + 4].bitcast(I32),
                 in_=scale_words[:, 4 * quadrant : 4 * quadrant + 4, :].rearrange("g r n -> r g n"),
             )
+        sin_rows = const.tile([P, TOKEN_TILES, D], BF16)
+        nc.sync.dma_start(out=sin_rows[:], in_=sin.rearrange("(p j) d -> p j d", j=TOKEN_TILES))
         nc.sync.dma_start(out=w_words_i32[:, :, row_words:], in_=w_source_i32[:, :, row_words:])
         for b in range(1, B):
             for g in range(PASSES):
@@ -97,6 +97,9 @@ def tile_lineartransformerblock_pa_kernel(tc, x, cos, sin, Wq_words, Wq_scales, 
 
         ident = const.tile([P, P], F32)
         make_identity(nc, ident[:])
+        nc.gpsimd.dma_start(out=bq_rows[0:H, :], in_=bq.rearrange("(h d) -> h d", d=D))
+        cos_rows = const.tile([P, TOKEN_TILES, D], BF16)
+        nc.gpsimd.dma_start(out=cos_rows[:], in_=cos.rearrange("(p j) d -> p j d", j=TOKEN_TILES))
         ident_bf = const.tile([P, P], BF16)
         nc.vector.tensor_copy(out=ident_bf[:], in_=ident[:])
         pair_swap = const.tile([P, P], F32)
@@ -146,11 +149,10 @@ def tile_lineartransformerblock_pa_kernel(tc, x, cos, sin, Wq_words, Wq_scales, 
                 out=x_codes[:, tokens].bitcast(FP8X4), scales=x_planes[:, tokens], in_=grouped_of[q][:]
             )
 
-        partner_rows = const.tile([P, TOKEN_TILES, D], BF16)
-        sin_pairs = sin_rows[:].rearrange("p j (i e) -> p (j i) e", e=2)
-        partner_pairs = partner_rows[:].rearrange("p j (i e) -> p (j i) e", e=2)
-        nc.vector.tensor_copy(out=partner_pairs[:, :, 0:1], in_=sin_pairs[:, :, 1:2])
-        nc.vector.tensor_scalar_mul(out=partner_pairs[:, :, 1:2], in0=sin_pairs[:, :, 0:1], scalar1=-1.0)
+        def keep_warm(count):
+            idle_ps = psum_rot.tile([P, P], F32, tag="rot")
+            for i in range(count):
+                nc.tensor.matmul(out=idle_ps[:], lhsT=zeros[:], rhs=zeros[:], start=True, stop=True)
 
         def turn_table(rows):
             table_ps = psum_rot.tile([P, S], BF16, tag="rot")
@@ -158,15 +160,11 @@ def tile_lineartransformerblock_pa_kernel(tc, x, cos, sin, Wq_words, Wq_scales, 
                 nc.tensor.transpose(table_ps[:, j * P : (j + 1) * P], rows[:, j, :], ident_bf[:])
             return table_ps
 
-        cos_tile = const.tile([P, S], BF16)
-        cos_ps = turn_table(cos_rows)
-        nc.scalar.copy(out=cos_tile[:], in_=cos_ps[:])
-        turn_quarter(0)
-        partner_tile = const.tile([P, S], BF16)
-        partner_ps = turn_table(partner_rows)
-        nc.vector.tensor_copy(out=partner_tile[:], in_=partner_ps[:])
-        cos_t = cos_tile[:]
-        partner_t = partner_tile[:]
+        keep_warm(WARM_BEFORE_X)
+        for q in range(QUARTERS):
+            turn_quarter(q)
+        quantise_quarter(0)
+        quantise_quarter(1)
 
         bias_ps = psum_rot.tile([P, len(ROW_HEADS) * D + H], F32, tag="rot")
         for i, h in enumerate(ROW_HEADS):
@@ -183,31 +181,23 @@ def tile_lineartransformerblock_pa_kernel(tc, x, cos, sin, Wq_words, Wq_scales, 
         bias_sb = const.tile([P, len(ROW_HEADS) * D + H], F32)
         nc.vector.tensor_copy(out=bias_sb[:], in_=bias_ps[:])
         bias = bias_sb[:, len(ROW_HEADS) * D :]
-        quantise_quarter(0)
+        quantise_quarter(2)
+        quantise_quarter(3)
 
-        def swapped(tile):
-            return tile[:].rearrange("p (i e) -> p i e", e=2)[:, :, ::-1]
+        cos_tile = const.tile([P, S], BF16)
+        cos_ps = turn_table(cos_rows)
+        nc.scalar.copy(out=cos_tile[:], in_=cos_ps[:])
+        cos_t = cos_tile[:]
+        partner_rows = const.tile([P, TOKEN_TILES, D], BF16)
+        sin_pairs = sin_rows[:].rearrange("p j (i e) -> p (j i) e", e=2)
+        partner_pairs = partner_rows[:].rearrange("p j (i e) -> p (j i) e", e=2)
+        nc.vector.tensor_copy(out=partner_pairs[:, :, 0:1], in_=sin_pairs[:, :, 1:2])
+        nc.vector.tensor_scalar_mul(out=partner_pairs[:, :, 1:2], in0=sin_pairs[:, :, 0:1], scalar1=-1.0)
+        partner_tile = const.tile([P, S], BF16)
+        partner_t = partner_tile[:]
 
         def pairs(tile):
             return tile[:].rearrange("p (i e) -> p i e", e=2)
-
-        roped_bias = {}
-        for i, h in enumerate(ROW_HEADS):
-            spread = bias_sb[:, i * D : (i + 1) * D].unsqueeze(1).to_broadcast([P, TOKEN_TILES, D])
-            direct = row_pool.tile([P, TOKEN_TILES * D], F32)
-            nc.gpsimd.tensor_tensor(
-                out=direct[:].rearrange("p (j d) -> p j d", d=D), in0=spread, in1=cos_rows[:], op=MULT
-            )
-            crossed = row_pool.tile([P, TOKEN_TILES * D], F32)
-            nc.gpsimd.tensor_tensor(
-                out=crossed[:].rearrange("p (j d) -> p j d", d=D), in0=spread, in1=partner_rows[:], op=MULT
-            )
-            total = const.tile([P, TOKEN_TILES * D], F32, name="roped_bias%d" % i)
-            nc.gpsimd.tensor_tensor(out=pairs(total), in0=pairs(direct), in1=swapped(crossed), op=ADD)
-            roped_bias[h] = total
-        for q in range(1, QUARTERS):
-            turn_quarter(q)
-            quantise_quarter(q)
 
         acc_of = {}
         made_of = {}
@@ -234,23 +224,35 @@ def tile_lineartransformerblock_pa_kernel(tc, x, cos, sin, Wq_words, Wq_scales, 
                     )
 
         def row_products(unit):
-            acc = acc_of[unit]
-            row_own = row_pool.tile([P, TOKEN_TILES * D], F32)
-            nc.vector.tensor_tensor(out=row_own[:], in0=acc[:], in1=cos_rows[:].rearrange("p j d -> p (j d)"), op=MULT)
-            row_other = row_pool.tile([P, TOKEN_TILES * D], F32)
+            i = ROW_HEADS.index(unit[1])
+            row_y = row_pool.tile([P, TOKEN_TILES, D], F32)
             nc.vector.tensor_tensor(
-                out=row_other[:], in0=acc[:], in1=partner_rows[:].rearrange("p j d -> p (j d)"), op=MULT
+                out=row_y[:],
+                in0=acc_of[unit][:].rearrange("p (j d) -> p j d", d=D),
+                in1=bias_sb[:, i * D : (i + 1) * D].unsqueeze(1).to_broadcast([P, TOKEN_TILES, D]),
+                op=ADD,
             )
-            row_part = row_pool.tile([P, TOKEN_TILES * D], F32)
-            nc.gpsimd.tensor_tensor(out=row_part[:], in0=row_own[:], in1=roped_bias[unit[1]][:], op=ADD)
+            row_own = row_pool.tile([P, TOKEN_TILES * D], F32)
+            nc.gpsimd.tensor_tensor(
+                out=row_own[:].rearrange("p (j d) -> p j d", d=D), in0=row_y[:], in1=cos_rows[:], op=MULT
+            )
+            row_other = row_pool.tile([P, TOKEN_TILES * D], F32)
+            nc.gpsimd.tensor_tensor(
+                out=row_other[:].rearrange("p (j d) -> p j d", d=D), in0=row_y[:], in1=partner_rows[:], op=MULT
+            )
             row_sum = row_pool.tile([P, TOKEN_TILES * D], F32)
-            nc.gpsimd.tensor_tensor(out=pairs(row_sum), in0=pairs(row_part), in1=swapped(row_other), op=ADD)
+            nc.gpsimd.tensor_tensor(
+                out=pairs(row_sum), in0=pairs(row_own), in1=pairs(row_other)[:, :, ::-1], op=ADD
+            )
             made_of[unit] = row_sum
 
-        def finish_rows(unit):
+        def finish_rows(unit, on_vector):
             b, h = unit
             res = res_pool.tile([P, TOKEN_TILES * D], F32)
-            nc.scalar.activation(out=res[:], in_=made_of[unit][:], func=RELU)
+            if on_vector:
+                nc.vector.tensor_scalar_max(out=res[:], in0=made_of[unit][:], scalar1=0.0)
+            else:
+                nc.scalar.activation(out=res[:], in_=made_of[unit][:], func=RELU)
             nc.sync.dma_start(out=out[b, h].rearrange("(p j) d -> p (j d)", j=TOKEN_TILES), in_=res[:])
 
         def multiply_pass(unit, g):
@@ -286,42 +288,74 @@ def tile_lineartransformerblock_pa_kernel(tc, x, cos, sin, Wq_words, Wq_scales, 
             )
             made_of[unit] = (own, other)
 
-        def finish(unit):
-            b, h = unit
+        def turn_back(rot, unit, rows):
             own, other = made_of[unit]
-            rot = psum_rot.tile([P, TOKEN_TILES, D], F32, tag="rot")
-            for j in range(TOKEN_TILES):
+            for i, j in enumerate(rows):
                 tokens = slice(j * P, (j + 1) * P)
                 nc.tensor.matmul(
-                    out=rot[:, j, :], lhsT=own[:, tokens], rhs=ident[:], is_transpose=True, start=True, stop=False
+                    out=rot[:, i, :], lhsT=own[:, tokens], rhs=ident[:], is_transpose=True, start=True, stop=False
                 )
                 nc.tensor.matmul(
-                    out=rot[:, j, :], lhsT=other[:, tokens], rhs=pair_swap[:], is_transpose=True, start=False, stop=True
+                    out=rot[:, i, :], lhsT=other[:, tokens], rhs=pair_swap[:], is_transpose=True, start=False, stop=True
                 )
+
+        def finish(unit):
+            b, h = unit
+            rot = psum_rot.tile([P, TOKEN_TILES, D], F32, tag="rot")
+            turn_back(rot, unit, range(TOKEN_TILES))
             res = res_pool.tile([P, TOKEN_TILES * D], F32)
             nc.scalar.activation(out=res[:], in_=rot[:].rearrange("p j d -> p (j d)"), func=RELU)
             nc.sync.dma_start(out=out[b, h].rearrange("(p j) d -> p (j d)", j=TOKEN_TILES), in_=res[:])
+
+        def finish_last(unit):
+            b, h = unit
+            for part in range(2):
+                rows = range(2 * part, 2 * part + 2)
+                rot_half = psum_rot.tile([P, 2, D], F32, tag="rot")
+                turn_back(rot_half, unit, rows)
+                res_half = res_pool.tile([P, 2 * D], F32)
+                source = rot_half[:].rearrange("p j d -> p (j d)")
+                if part == 0:
+                    nc.scalar.activation(out=res_half[:], in_=source, func=RELU)
+                else:
+                    nc.vector.tensor_scalar_max(out=res_half[:], in0=source, scalar1=0.0)
+                nc.sync.dma_start(
+                    out=out[b, h].rearrange("(p j) d -> p j d", j=TOKEN_TILES)[:, 2 * part : 2 * part + 2, :],
+                    in_=res_half[:].rearrange("p (j d) -> p j d", d=D),
+                )
 
         for n in range(ROUNDS + 1):
             turning = quarters_of_round(n)
             for q in turning:
                 sort_quarter(q)
+            if n >= 1:
+                for q in quarters_of_round(n - 1):
+                    quantise_quarter(q)
             if n < ROUNDS:
                 if n > 0:
                     open_banks(n)
                 row_unit = round_units(n)[0]
                 multiply_rows(row_unit)
                 row_products(row_unit)
+                if n == 0:
+                    partner_ps = turn_table(partner_rows)
+                    nc.scalar.copy(out=partner_tile[:], in_=partner_ps[:])
                 for unit in round_units(n)[1:]:
                     for g in range(PASSES):
                         if n > 0 or g > 0:
                             multiply_pass(unit, g)
                     products(unit)
             if n >= 1:
-                for unit in round_units(n - 1)[1:]:
-                    finish(unit)
+                before = round_units(n - 1)
+                if n < ROUNDS:
+                    finish(before[1])
+                    finish_rows(before[0], on_vector=False)
+                    for unit in before[2:]:
+                        finish(unit)
+                else:
+                    for unit in before[1:-1]:
+                        finish(unit)
+                    finish_rows(before[0], on_vector=True)
+                    finish_last(before[-1])
             for q in turning:
                 turn_quarter(q)
-                quantise_quarter(q)
-            if n < ROUNDS:
-                finish_rows(row_unit)

@@ -50,7 +50,7 @@ def tile_lineartransformerblock_pa_kernel(tc, x, cos, sin, Wq_words, Wq_scales, 
         stage = ctx.enter_context(tc.tile_pool(name="stage", bufs=4))
         mx_pool = ctx.enter_context(tc.tile_pool(name="mx_pool", bufs=2 * PASSES))
         prod_pool = ctx.enter_context(tc.tile_pool(name="prod_pool", bufs=2 * GROUP))
-        row_pool = ctx.enter_context(tc.tile_pool(name="row_pool", bufs=2))
+        row_pool = ctx.enter_context(tc.tile_pool(name="row_pool", bufs=3))
         res_pool = ctx.enter_context(tc.tile_pool(name="res_pool", bufs=8))
         psum_acc = ctx.enter_context(tc.psum_pool(name="psum_acc", bufs=4))
         psum_rot = ctx.enter_context(tc.psum_pool(name="psum_rot", bufs=4))
@@ -88,6 +88,8 @@ def tile_lineartransformerblock_pa_kernel(tc, x, cos, sin, Wq_words, Wq_scales, 
                 out=w_planes[32 * quadrant : 32 * quadrant + 4].bitcast(I32),
                 in_=scale_words[:, 4 * quadrant : 4 * quadrant + 4, :].rearrange("g r n -> r g n"),
             )
+        cos_rows = const.tile([P, TOKEN_TILES, D], BF16)
+        nc.sync.dma_start(out=cos_rows[:], in_=cos.rearrange("(p j) d -> p j d", j=TOKEN_TILES))
         sin_rows = const.tile([P, TOKEN_TILES, D], BF16)
         nc.sync.dma_start(out=sin_rows[:], in_=sin.rearrange("(p j) d -> p j d", j=TOKEN_TILES))
         nc.sync.dma_start(out=w_words_i32[:, :, row_words:], in_=w_source_i32[:, :, row_words:])
@@ -98,8 +100,6 @@ def tile_lineartransformerblock_pa_kernel(tc, x, cos, sin, Wq_words, Wq_scales, 
         ident = const.tile([P, P], F32)
         make_identity(nc, ident[:])
         nc.gpsimd.dma_start(out=bq_rows[0:H, :], in_=bq.rearrange("(h d) -> h d", d=D))
-        cos_rows = const.tile([P, TOKEN_TILES, D], BF16)
-        nc.gpsimd.dma_start(out=cos_rows[:], in_=cos.rearrange("(p j) d -> p j d", j=TOKEN_TILES))
         ident_bf = const.tile([P, P], BF16)
         nc.vector.tensor_copy(out=ident_bf[:], in_=ident[:])
         pair_swap = const.tile([P, P], F32)
@@ -326,7 +326,7 @@ def tile_lineartransformerblock_pa_kernel(tc, x, cos, sin, Wq_words, Wq_scales, 
 
         for n in range(ROUNDS + 1):
             turning = quarters_of_round(n)
-            for q in turning:
+            for q in turning[:2]:
                 sort_quarter(q)
             if n >= 1:
                 for q in quarters_of_round(n - 1):
@@ -340,6 +340,8 @@ def tile_lineartransformerblock_pa_kernel(tc, x, cos, sin, Wq_words, Wq_scales, 
                 if n == 0:
                     partner_ps = turn_table(partner_rows)
                     nc.scalar.copy(out=partner_tile[:], in_=partner_ps[:])
+                    for q in turning[2:]:
+                        sort_quarter(q)
                 for unit in round_units(n)[1:]:
                     for g in range(PASSES):
                         if n > 0 or g > 0:
@@ -348,9 +350,7 @@ def tile_lineartransformerblock_pa_kernel(tc, x, cos, sin, Wq_words, Wq_scales, 
             if n >= 1:
                 before = round_units(n - 1)
                 if n < ROUNDS:
-                    finish(before[1])
-                    finish_rows(before[0], on_vector=False)
-                    for unit in before[2:]:
+                    for unit in before[1:]:
                         finish(unit)
                 else:
                     for unit in before[1:-1]:
@@ -359,3 +359,5 @@ def tile_lineartransformerblock_pa_kernel(tc, x, cos, sin, Wq_words, Wq_scales, 
                     finish_last(before[-1])
             for q in turning:
                 turn_quarter(q)
+            if 1 <= n < ROUNDS:
+                finish_rows(before[0], on_vector=False)

@@ -21,9 +21,8 @@ PACK = 4
 K_PASS = P * PACK
 PASSES = C // K_PASS
 TOKEN_TILES = S // P
-QUARTERS = 2 * PASSES
 HALF = S // 2
-UNSORTED = QUARTERS
+SORTED_FROM = 2
 
 FLOPS = 2 * B * S * C * E
 
@@ -34,10 +33,11 @@ WARM_BEFORE_X = 15
 ROW_HEADS = [0, GROUP]
 
 
-def quarters_of_round(n):
+def passes_of_round(n):
     if n == 0:
-        return list(range(QUARTERS, 2 * QUARTERS))
-    return [q for q in (2 * n + 6, 2 * n + 7) if q < B * QUARTERS]
+        return [(1, g) for g in range(PASSES)]
+    b, g = divmod(n + 3, PASSES)
+    return [(b, g)] if b < B else []
 
 
 def tile_lineartransformerblock_pa_kernel(tc, x, cos, sin, Wq_words, Wq_scales, bq, out):
@@ -46,9 +46,9 @@ def tile_lineartransformerblock_pa_kernel(tc, x, cos, sin, Wq_words, Wq_scales, 
         ctx.enter_context(tc.manual_schedule())
         const = ctx.enter_context(tc.tile_pool(name="const", bufs=1))
         x_pool = ctx.enter_context(tc.tile_pool(name="x_pool", bufs=B * PASSES))
-        sort_pool = ctx.enter_context(tc.tile_pool(name="sort_pool", bufs=QUARTERS))
+        sort_pool = ctx.enter_context(tc.tile_pool(name="sort_pool", bufs=2))
         stage = ctx.enter_context(tc.tile_pool(name="stage", bufs=4))
-        mx_pool = ctx.enter_context(tc.tile_pool(name="mx_pool", bufs=2 * PASSES))
+        mx_pool = ctx.enter_context(tc.tile_pool(name="mx_pool", bufs=3 * PASSES))
         prod_pool = ctx.enter_context(tc.tile_pool(name="prod_pool", bufs=2 * GROUP))
         row_pool = ctx.enter_context(tc.tile_pool(name="row_pool", bufs=3))
         res_pool = ctx.enter_context(tc.tile_pool(name="res_pool", bufs=8))
@@ -112,41 +112,42 @@ def tile_lineartransformerblock_pa_kernel(tc, x, cos, sin, Wq_words, Wq_scales, 
         grouped_of = {}
         mx_of = {}
 
-        def quarter_words(q):
-            b, g, half = q // QUARTERS, (q % QUARTERS) // 2, q % 2
-            rows = x_tiles[(b, g)][:, 2 * half : 2 * half + 2, :]
-            return rows.bitcast(F32).rearrange("p j (q u) -> p j u q", u=2)
+        def words_of(b, g):
+            return x_tiles[(b, g)][:].bitcast(F32).rearrange("p j (q u) -> p j u q", u=2)
 
-        def sort_quarter(q):
-            x_sorted = sort_pool.tile([P, 2, 2, P], F32)
-            nc.scalar.copy(out=x_sorted[:], in_=quarter_words(q))
-            sorted_of[q] = x_sorted[:]
+        def sort_pass(b, g):
+            x_sorted = sort_pool.tile([P, TOKEN_TILES, 2, P], F32)
+            nc.scalar.copy(out=x_sorted[:], in_=words_of(b, g))
+            sorted_of[(b, g)] = x_sorted
 
-        def turn_quarter(q):
-            if q < UNSORTED:
-                words = quarter_words(q)
-            else:
-                words = sorted_of[q]
-            xt = psum_rot.tile([P, 2, 2 * P], F32, tag="rot")
-            for u in range(2):
-                for jj in range(2):
-                    nc.tensor.transpose(xt[:, u, jj * P : (jj + 1) * P], words[:, jj, u, :], ident[:])
-            grouped = stage.tile([P, HALF * PACK], BF16, align_bytes=64)
-            nc.scalar.copy(
-                out=grouped[:].bitcast(F32).rearrange("q (n u) -> q n u", u=2), in_=xt[:].rearrange("q u n -> q n u")
-            )
-            grouped_of[q] = grouped
+        def turn_pass(b, g):
+            words = sorted_of[(b, g)][:] if (b, g) in sorted_of else words_of(b, g)
+            grouped = stage.tile([P, S * PACK], BF16, align_bytes=64)
+            grouped_of[(b, g)] = grouped
+            for half in range(2):
+                xt = psum_rot.tile([P, 2, 2 * P], F32, tag="rot")
+                for u in range(2):
+                    for jj in range(2):
+                        nc.tensor.transpose(
+                            xt[:, u, jj * P : (jj + 1) * P], words[:, 2 * half + jj, u, :], ident[:]
+                        )
+                columns = slice(HALF * PACK * half, HALF * PACK * (half + 1))
+                nc.scalar.copy(
+                    out=grouped[:, columns].bitcast(F32).rearrange("q (n u) -> q n u", u=2),
+                    in_=xt[:].rearrange("q u n -> q n u"),
+                )
 
-        def quantise_quarter(q):
-            b, g, half = q // QUARTERS, (q % QUARTERS) // 2, q % 2
-            if half == 0:
+        def quantise(b, g, first, count):
+            if (b, g) not in mx_of:
                 x_codes = mx_pool.tile([P, S], U32, align_bytes=64)
                 x_planes = mx_pool.tile([P, S], U8, align_bytes=64)
                 mx_of[(b, g)] = (x_codes, x_planes)
             x_codes, x_planes = mx_of[(b, g)]
-            tokens = slice(HALF * half, HALF * (half + 1))
+            tokens = slice(P * first, P * (first + count))
             nc.vector.quantize_mx(
-                out=x_codes[:, tokens].bitcast(FP8X4), scales=x_planes[:, tokens], in_=grouped_of[q][:]
+                out=x_codes[:, tokens].bitcast(FP8X4),
+                scales=x_planes[:, tokens],
+                in_=grouped_of[(b, g)][:, PACK * P * first : PACK * P * (first + count)],
             )
 
         def keep_warm(count):
@@ -161,10 +162,10 @@ def tile_lineartransformerblock_pa_kernel(tc, x, cos, sin, Wq_words, Wq_scales, 
             return table_ps
 
         keep_warm(WARM_BEFORE_X)
-        for q in range(QUARTERS):
-            turn_quarter(q)
-        quantise_quarter(0)
-        quantise_quarter(1)
+        for g in range(PASSES):
+            turn_pass(0, g)
+        quantise(0, 0, 0, 2)
+        quantise(0, 0, 2, 2)
 
         bias_ps = psum_rot.tile([P, len(ROW_HEADS) * D + H], F32, tag="rot")
         for i, h in enumerate(ROW_HEADS):
@@ -181,20 +182,17 @@ def tile_lineartransformerblock_pa_kernel(tc, x, cos, sin, Wq_words, Wq_scales, 
         bias_sb = const.tile([P, len(ROW_HEADS) * D + H], F32)
         nc.vector.tensor_copy(out=bias_sb[:], in_=bias_ps[:])
         bias = bias_sb[:, len(ROW_HEADS) * D :]
-        quantise_quarter(2)
-        quantise_quarter(3)
+        quantise(0, 1, 0, 2)
+        quantise(0, 1, 2, 2)
 
-        cos_tile = const.tile([P, S], BF16)
+        tables_t = const.tile([P, 2, S], BF16)
         cos_ps = turn_table(cos_rows)
-        nc.scalar.copy(out=cos_tile[:], in_=cos_ps[:])
-        cos_t = cos_tile[:]
+        nc.scalar.copy(out=tables_t[:, 0, :], in_=cos_ps[:])
         partner_rows = const.tile([P, TOKEN_TILES, D], BF16)
         sin_pairs = sin_rows[:].rearrange("p j (i e) -> p (j i) e", e=2)
         partner_pairs = partner_rows[:].rearrange("p j (i e) -> p (j i) e", e=2)
         nc.vector.tensor_copy(out=partner_pairs[:, :, 0:1], in_=sin_pairs[:, :, 1:2])
         nc.vector.tensor_scalar_mul(out=partner_pairs[:, :, 1:2], in0=sin_pairs[:, :, 0:1], scalar1=-1.0)
-        partner_tile = const.tile([P, S], BF16)
-        partner_t = partner_tile[:]
 
         def pairs(tile):
             return tile[:].rearrange("p (i e) -> p i e", e=2)
@@ -277,16 +275,16 @@ def tile_lineartransformerblock_pa_kernel(tc, x, cos, sin, Wq_words, Wq_scales, 
 
         def products(unit):
             b, h = unit
-            acc = acc_of[unit]
-            own = prod_pool.tile([P, S], F32)
+            both = prod_pool.tile([P, 2, S], F32)
             nc.vector.scalar_tensor_tensor(
-                out=own[:], in0=acc[:], scalar=bias[:, h : h + 1], in1=cos_t, op0=ADD, op1=MULT
+                out=both[:],
+                in0=acc_of[unit][:].unsqueeze(1).to_broadcast([P, 2, S]),
+                scalar=bias[:, h : h + 1],
+                in1=tables_t[:],
+                op0=ADD,
+                op1=MULT,
             )
-            other = prod_pool.tile([P, S], F32)
-            nc.vector.scalar_tensor_tensor(
-                out=other[:], in0=acc[:], scalar=bias[:, h : h + 1], in1=partner_t, op0=ADD, op1=MULT
-            )
-            made_of[unit] = (own, other)
+            made_of[unit] = (both[:, 0, :], both[:, 1, :])
 
         def turn_back(rot, unit, rows):
             own, other = made_of[unit]
@@ -325,12 +323,13 @@ def tile_lineartransformerblock_pa_kernel(tc, x, cos, sin, Wq_words, Wq_scales, 
                 )
 
         for n in range(ROUNDS + 1):
-            turning = quarters_of_round(n)
-            for q in turning[:2]:
-                sort_quarter(q)
+            turning = passes_of_round(n)
+            for b, g in turning:
+                if b >= SORTED_FROM:
+                    sort_pass(b, g)
             if n >= 1:
-                for q in quarters_of_round(n - 1):
-                    quantise_quarter(q)
+                for b, g in passes_of_round(n - 1):
+                    quantise(b, g, 0, TOKEN_TILES)
             if n < ROUNDS:
                 if n > 0:
                     open_banks(n)
@@ -339,9 +338,7 @@ def tile_lineartransformerblock_pa_kernel(tc, x, cos, sin, Wq_words, Wq_scales, 
                 row_products(row_unit)
                 if n == 0:
                     partner_ps = turn_table(partner_rows)
-                    nc.scalar.copy(out=partner_tile[:], in_=partner_ps[:])
-                    for q in turning[2:]:
-                        sort_quarter(q)
+                    nc.scalar.copy(out=tables_t[:, 1, :], in_=partner_ps[:])
                 for unit in round_units(n)[1:]:
                     for g in range(PASSES):
                         if n > 0 or g > 0:
@@ -357,7 +354,7 @@ def tile_lineartransformerblock_pa_kernel(tc, x, cos, sin, Wq_words, Wq_scales, 
                         finish(unit)
                     finish_rows(before[0], on_vector=True)
                     finish_last(before[-1])
-            for q in turning:
-                turn_quarter(q)
+            for b, g in turning:
+                turn_pass(b, g)
             if 1 <= n < ROUNDS:
                 finish_rows(before[0], on_vector=False)

@@ -59,7 +59,7 @@ def tile_lineartransformerblock_pa_kernel(tc, x, cos, sin, Wq_words, Wq_scales, 
         nc.vector.memset(zeros[:], 0.0)
         bq_rows = const.tile([P, P], BF16)
         nc.vector.memset(bq_rows[:], 0.0)
-        w_planes = const.tile([P, PASSES, E], U8, align_bytes=64)
+        w_planes = const.tile([P, PASSES, E], U8, align_bytes=256)
         nc.vector.memset(w_planes[:].bitcast(I32), 0)
 
         x_tiles = {}
@@ -73,7 +73,7 @@ def tile_lineartransformerblock_pa_kernel(tc, x, cos, sin, Wq_words, Wq_scales, 
                 in_=x[b].rearrange("(p j) c -> p j c", j=TOKEN_TILES)[:, rows, K_PASS * g : K_PASS * (g + 1)],
             )
 
-        w_words = const.tile([P, PASSES, 2 * E], U8, align_bytes=64)
+        w_words = const.tile([P, PASSES, 2 * E], U8, align_bytes=256)
         w_words_i32 = w_words[:].bitcast(I32)
         w_source_i32 = Wq_words.bitcast(I32).rearrange("g p n -> p g n")
         row_words = E // 4
@@ -139,8 +139,8 @@ def tile_lineartransformerblock_pa_kernel(tc, x, cos, sin, Wq_words, Wq_scales, 
 
         def quantise(b, g, first, count):
             if (b, g) not in mx_of:
-                x_codes = mx_pool.tile([P, S], U32, align_bytes=64)
-                x_planes = mx_pool.tile([P, S], U8, align_bytes=64)
+                x_codes = mx_pool.tile([P, S], U32, align_bytes=256)
+                x_planes = mx_pool.tile([P, S], U8, align_bytes=256)
                 mx_of[(b, g)] = (x_codes, x_planes)
             x_codes, x_planes = mx_of[(b, g)]
             tokens = slice(P * first, P * (first + count))

@@ -13,6 +13,7 @@ FP4X4 = mybir.dt.float4_e2m1fn_x4
 ADD = mybir.AluOpType.add
 MULT = mybir.AluOpType.mult
 RELU = mybir.ActivationFunctionType.Relu
+IDENTITY = mybir.ActivationFunctionType.Identity
 
 B, S, C, H, D = 4, 512, 1024, 8, 128
 E = H * D
@@ -33,6 +34,14 @@ WARM_BEFORE_X = 15
 ROW_HEADS = [0, GROUP]
 
 
+def row_count(n):
+    return 1 if n < ROUNDS - 1 else 0
+
+
+def turned_count(n):
+    return 1 if 1 <= n < ROUNDS - 2 else 0
+
+
 def passes_of_round(n):
     if n == 0:
         return [(1, g) for g in range(PASSES)]
@@ -50,6 +59,7 @@ def tile_lineartransformerblock_pa_kernel(tc, x, cos, sin, Wq_words, Wq_scales, 
         stage = ctx.enter_context(tc.tile_pool(name="stage", bufs=4))
         mx_pool = ctx.enter_context(tc.tile_pool(name="mx_pool", bufs=3 * PASSES))
         prod_pool = ctx.enter_context(tc.tile_pool(name="prod_pool", bufs=2 * GROUP))
+        lift_pool = ctx.enter_context(tc.tile_pool(name="lift_pool", bufs=2))
         row_pool = ctx.enter_context(tc.tile_pool(name="row_pool", bufs=3))
         res_pool = ctx.enter_context(tc.tile_pool(name="res_pool", bufs=8))
         psum_acc = ctx.enter_context(tc.psum_pool(name="psum_acc", bufs=4))
@@ -88,8 +98,10 @@ def tile_lineartransformerblock_pa_kernel(tc, x, cos, sin, Wq_words, Wq_scales, 
                 out=w_planes[32 * quadrant : 32 * quadrant + 4].bitcast(I32),
                 in_=scale_words[:, 4 * quadrant : 4 * quadrant + 4, :].rearrange("g r n -> r g n"),
             )
-        cos_rows = const.tile([P, TOKEN_TILES, D], BF16)
-        nc.sync.dma_start(out=cos_rows[:], in_=cos.rearrange("(p j) d -> p j d", j=TOKEN_TILES))
+        tables_rows = const.tile([P, 2, TOKEN_TILES, D], BF16)
+        cos_rows = tables_rows[:, 0]
+        partner_rows = tables_rows[:, 1]
+        nc.sync.dma_start(out=cos_rows, in_=cos.rearrange("(p j) d -> p j d", j=TOKEN_TILES))
         sin_rows = const.tile([P, TOKEN_TILES, D], BF16)
         nc.sync.dma_start(out=sin_rows[:], in_=sin.rearrange("(p j) d -> p j d", j=TOKEN_TILES))
         nc.sync.dma_start(out=w_words_i32[:, :, row_words:], in_=w_source_i32[:, :, row_words:])
@@ -188,9 +200,8 @@ def tile_lineartransformerblock_pa_kernel(tc, x, cos, sin, Wq_words, Wq_scales, 
         tables_t = const.tile([P, 2, S], BF16)
         cos_ps = turn_table(cos_rows)
         nc.scalar.copy(out=tables_t[:, 0, :], in_=cos_ps[:])
-        partner_rows = const.tile([P, TOKEN_TILES, D], BF16)
         sin_pairs = sin_rows[:].rearrange("p j (i e) -> p (j i) e", e=2)
-        partner_pairs = partner_rows[:].rearrange("p j (i e) -> p (j i) e", e=2)
+        partner_pairs = partner_rows.rearrange("p j (i e) -> p (j i) e", e=2)
         nc.vector.tensor_copy(out=partner_pairs[:, :, 0:1], in_=sin_pairs[:, :, 1:2])
         nc.vector.tensor_scalar_mul(out=partner_pairs[:, :, 1:2], in0=sin_pairs[:, :, 0:1], scalar1=-1.0)
 
@@ -198,7 +209,17 @@ def tile_lineartransformerblock_pa_kernel(tc, x, cos, sin, Wq_words, Wq_scales, 
             return tile[:].rearrange("p (i e) -> p i e", e=2)
 
         acc_of = {}
+        lifted_of = {}
         made_of = {}
+
+        def row_units(n):
+            return round_units(n)[: row_count(n)]
+
+        def turned_units(n):
+            return round_units(n)[row_count(n) : row_count(n) + turned_count(n)]
+
+        def column_units(n):
+            return round_units(n)[row_count(n) + turned_count(n) :]
 
         def open_banks(n):
             for unit in round_units(n):
@@ -232,11 +253,11 @@ def tile_lineartransformerblock_pa_kernel(tc, x, cos, sin, Wq_words, Wq_scales, 
             )
             row_own = row_pool.tile([P, TOKEN_TILES * D], F32)
             nc.gpsimd.tensor_tensor(
-                out=row_own[:].rearrange("p (j d) -> p j d", d=D), in0=row_y[:], in1=cos_rows[:], op=MULT
+                out=row_own[:].rearrange("p (j d) -> p j d", d=D), in0=row_y[:], in1=cos_rows, op=MULT
             )
             row_other = row_pool.tile([P, TOKEN_TILES * D], F32)
             nc.gpsimd.tensor_tensor(
-                out=row_other[:].rearrange("p (j d) -> p j d", d=D), in0=row_y[:], in1=partner_rows[:], op=MULT
+                out=row_other[:].rearrange("p (j d) -> p j d", d=D), in0=row_y[:], in1=partner_rows, op=MULT
             )
             row_sum = row_pool.tile([P, TOKEN_TILES * D], F32)
             nc.gpsimd.tensor_tensor(
@@ -270,7 +291,7 @@ def tile_lineartransformerblock_pa_kernel(tc, x, cos, sin, Wq_words, Wq_scales, 
             return [(unit // H, unit % H) for unit in range(GROUP * n, GROUP * (n + 1))]
 
         open_banks(0)
-        for unit in round_units(0)[1:]:
+        for unit in column_units(0):
             multiply_pass(unit, 0)
 
         def products(unit):
@@ -285,6 +306,31 @@ def tile_lineartransformerblock_pa_kernel(tc, x, cos, sin, Wq_words, Wq_scales, 
                 op1=MULT,
             )
             made_of[unit] = (both[:, 0, :], both[:, 1, :])
+
+        def lift(unit):
+            y_sb = lift_pool.tile([P, S], F32)
+            nc.scalar.activation(out=y_sb[:], in_=acc_of[unit][:], func=IDENTITY, bias=bias[:, unit[1] : unit[1] + 1])
+            lifted_of[unit] = y_sb
+
+        def turn_lifted(unit):
+            rot = psum_rot.tile([P, TOKEN_TILES, D], F32, tag="rot")
+            for j in range(TOKEN_TILES):
+                nc.tensor.transpose(rot[:, j, :], lifted_of[unit][:, j * P : (j + 1) * P], ident[:])
+            lifted_of[unit] = rot
+
+        def turned_products(unit):
+            both = row_pool.tile([P, 2, TOKEN_TILES * D], F32)
+            nc.vector.tensor_tensor(
+                out=both[:],
+                in0=lifted_of[unit][:].rearrange("p j d -> p (j d)").unsqueeze(1).to_broadcast([P, 2, TOKEN_TILES * D]),
+                in1=tables_rows[:].rearrange("p t j d -> p t (j d)"),
+                op=MULT,
+            )
+            turned_sum = row_pool.tile([P, TOKEN_TILES * D], F32)
+            own_pairs = both[:, 0, :].rearrange("p (i e) -> p i e", e=2)
+            other_pairs = both[:, 1, :].rearrange("p (i e) -> p i e", e=2)
+            nc.gpsimd.tensor_tensor(out=pairs(turned_sum), in0=own_pairs, in1=other_pairs[:, :, ::-1], op=ADD)
+            made_of[unit] = turned_sum
 
         def turn_back(rot, unit, rows):
             own, other = made_of[unit]
@@ -328,33 +374,43 @@ def tile_lineartransformerblock_pa_kernel(tc, x, cos, sin, Wq_words, Wq_scales, 
                 if b >= SORTED_FROM:
                     sort_pass(b, g)
             if n >= 1:
+                for unit in turned_units(n - 1):
+                    turned_products(unit)
                 for b, g in passes_of_round(n - 1):
                     quantise(b, g, 0, TOKEN_TILES)
             if n < ROUNDS:
                 if n > 0:
                     open_banks(n)
-                row_unit = round_units(n)[0]
-                multiply_rows(row_unit)
-                row_products(row_unit)
+                for unit in row_units(n):
+                    multiply_rows(unit)
+                    row_products(unit)
                 if n == 0:
                     partner_ps = turn_table(partner_rows)
                     nc.scalar.copy(out=tables_t[:, 1, :], in_=partner_ps[:])
-                for unit in round_units(n)[1:]:
+                for unit in turned_units(n):
+                    for g in range(PASSES):
+                        multiply_pass(unit, g)
+                    lift(unit)
+                for unit in column_units(n):
                     for g in range(PASSES):
                         if n > 0 or g > 0:
                             multiply_pass(unit, g)
                     products(unit)
             if n >= 1:
-                before = round_units(n - 1)
+                before = column_units(n - 1)
                 if n < ROUNDS:
-                    for unit in before[1:]:
+                    for unit in before:
                         finish(unit)
                 else:
-                    for unit in before[1:-1]:
+                    for unit in before[:-1]:
                         finish(unit)
-                    finish_rows(before[0], on_vector=True)
+                    for unit in row_units(n - 2):
+                        finish_rows(unit, on_vector=True)
                     finish_last(before[-1])
             for b, g in turning:
                 turn_pass(b, g)
-            if 1 <= n < ROUNDS:
-                finish_rows(before[0], on_vector=False)
+            for unit in turned_units(n):
+                turn_lifted(unit)
+            if 1 <= n < ROUNDS - 1:
+                for unit in row_units(n - 1) + turned_units(n - 1):
+                    finish_rows(unit, on_vector=False)

@@ -23,7 +23,6 @@ K_PASS = P * PACK
 PASSES = C // K_PASS
 TOKEN_TILES = S // P
 HALF = S // 2
-SORTED_FROM = 2
 
 FLOPS = 2 * B * S * C * E
 
@@ -371,7 +370,7 @@ def tile_lineartransformerblock_pa_kernel(tc, x, cos, sin, Wq_words, Wq_scales, 
         for n in range(ROUNDS + 1):
             turning = passes_of_round(n)
             for b, g in turning:
-                if b >= SORTED_FROM:
+                if n > 0 or g == 0:
                     sort_pass(b, g)
             if n >= 1:
                 for unit in turned_units(n - 1):
@@ -387,6 +386,7 @@ def tile_lineartransformerblock_pa_kernel(tc, x, cos, sin, Wq_words, Wq_scales, 
                 if n == 0:
                     partner_ps = turn_table(partner_rows)
                     nc.scalar.copy(out=tables_t[:, 1, :], in_=partner_ps[:])
+                    sort_pass(1, 1)
                 for unit in turned_units(n):
                     for g in range(PASSES):
                         multiply_pass(unit, g)

from contextlib import ExitStack

import concourse.mybir as mybir
from concourse.masks import make_identity

F32 = mybir.dt.float32
BF16 = mybir.dt.bfloat16
I32 = mybir.dt.int32
U8 = mybir.dt.uint8
U32 = mybir.dt.uint32
FP8X4 = mybir.dt.float8_e4m3fn_x4
FP4X4 = mybir.dt.float4_e2m1fn_x4
ADD = mybir.AluOpType.add
MULT = mybir.AluOpType.mult
RELU = mybir.ActivationFunctionType.Relu
IDENTITY = mybir.ActivationFunctionType.Identity

B, S, C, H, D = 4, 512, 1024, 8, 128
E = H * D
P = 128
PACK = 4
K_PASS = P * PACK
PASSES = C // K_PASS
TOKEN_TILES = S // P
HALF = S // 2

FLOPS = 2 * B * S * C * E


GROUP = 4
ROUNDS = B * H // GROUP
WARM_BEFORE_X = 15
ROW_HEADS = [0, GROUP]


def row_count(n):
    return 1 if n < ROUNDS - 1 else 0


def turned_count(n):
    return 1 if 1 <= n < ROUNDS - 2 else 0


def passes_of_round(n):
    if n == 0:
        return [(1, g) for g in range(PASSES)]
    b, g = divmod(n + 3, PASSES)
    return [(b, g)] if b < B else []


def tile_lineartransformerblock_pa_kernel(tc, x, cos, sin, Wq_words, Wq_scales, bq, out):
    nc = tc.nc
    with ExitStack() as ctx:
        ctx.enter_context(tc.manual_schedule())
        const = ctx.enter_context(tc.tile_pool(name="const", bufs=1))
        x_pool = ctx.enter_context(tc.tile_pool(name="x_pool", bufs=B * PASSES))
        sort_pool = ctx.enter_context(tc.tile_pool(name="sort_pool", bufs=2))
        stage = ctx.enter_context(tc.tile_pool(name="stage", bufs=4))
        mx_pool = ctx.enter_context(tc.tile_pool(name="mx_pool", bufs=3 * PASSES))
        prod_pool = ctx.enter_context(tc.tile_pool(name="prod_pool", bufs=2 * GROUP))
        lift_pool = ctx.enter_context(tc.tile_pool(name="lift_pool", bufs=2))
        row_pool = ctx.enter_context(tc.tile_pool(name="row_pool", bufs=3))
        res_pool = ctx.enter_context(tc.tile_pool(name="res_pool", bufs=8))
        psum_acc = ctx.enter_context(tc.psum_pool(name="psum_acc", bufs=4))
        psum_rot = ctx.enter_context(tc.psum_pool(name="psum_rot", bufs=4))

        zeros = const.tile([P, P], BF16)
        nc.vector.memset(zeros[:], 0.0)
        bq_rows = const.tile([P, P], BF16)
        nc.vector.memset(bq_rows[:], 0.0)
        w_planes = const.tile([P, PASSES, E], U8, align_bytes=256)
        nc.vector.memset(w_planes[:].bitcast(I32), 0)

        x_tiles = {}

        def load_x(b, g, rows):
            if (b, g) not in x_tiles:
                x_sb = x_pool.tile([P, TOKEN_TILES, K_PASS], BF16)
                x_tiles[(b, g)] = x_sb
            nc.sync.dma_start(
                out=x_tiles[(b, g)][:, rows, :],
                in_=x[b].rearrange("(p j) c -> p j c", j=TOKEN_TILES)[:, rows, K_PASS * g : K_PASS * (g + 1)],
            )

        w_words = const.tile([P, PASSES, 2 * E], U8, align_bytes=256)
        w_words_i32 = w_words[:].bitcast(I32)
        w_source_i32 = Wq_words.bitcast(I32).rearrange("g p n -> p g n")
        row_words = E // 4
        scale_words = Wq_scales.bitcast(I32)

        load_x(0, 0, slice(0, 2))
        load_x(0, 0, slice(2, 4))
        load_x(0, 1, slice(0, 4))
        nc.sync.dma_start(out=w_words_i32[:, :, 0:row_words], in_=w_source_i32[:, :, 0:row_words])
        for quadrant in range(4):
            nc.sync.dma_start(
                out=w_planes[32 * quadrant : 32 * quadrant + 4].bitcast(I32),
                in_=scale_words[:, 4 * quadrant : 4 * quadrant + 4, :].rearrange("g r n -> r g n"),
            )
        tables_rows = const.tile([P, 2, TOKEN_TILES, D], BF16)
        cos_rows = tables_rows[:, 0]
        partner_rows = tables_rows[:, 1]
        nc.sync.dma_start(out=cos_rows, in_=cos.rearrange("(p j) d -> p j d", j=TOKEN_TILES))
        sin_rows = const.tile([P, TOKEN_TILES, D], BF16)
        nc.sync.dma_start(out=sin_rows[:], in_=sin.rearrange("(p j) d -> p j d", j=TOKEN_TILES))
        nc.sync.dma_start(out=w_words_i32[:, :, row_words:], in_=w_source_i32[:, :, row_words:])
        for b in range(1, B):
            for g in range(PASSES):
                load_x(b, g, slice(0, 4))

        ident = const.tile([P, P], F32)
        make_identity(nc, ident[:])
        nc.gpsimd.dma_start(out=bq_rows[0:H, :], in_=bq.rearrange("(h d) -> h d", d=D))
        ident_bf = const.tile([P, P], BF16)
        nc.vector.tensor_copy(out=ident_bf[:], in_=ident[:])
        pair_swap = const.tile([P, P], F32)
        ident_pairs = ident[:].rearrange("p (i e) -> p i e", e=2)
        swap_pairs = pair_swap[:].rearrange("p (i e) -> p i e", e=2)
        nc.vector.tensor_copy(out=swap_pairs[:, :, 0:1], in_=ident_pairs[:, :, 1:2])
        nc.vector.tensor_copy(out=swap_pairs[:, :, 1:2], in_=ident_pairs[:, :, 0:1])

        sorted_of = {}
        grouped_of = {}
        mx_of = {}

        def words_of(b, g):
            return x_tiles[(b, g)][:].bitcast(F32).rearrange("p j (q u) -> p j u q", u=2)

        def sort_pass(b, g):
            x_sorted = sort_pool.tile([P, TOKEN_TILES, 2, P], F32)
            nc.scalar.copy(out=x_sorted[:], in_=words_of(b, g))
            sorted_of[(b, g)] = x_sorted

        def turn_pass(b, g):
            words = sorted_of[(b, g)][:] if (b, g) in sorted_of else words_of(b, g)
            grouped = stage.tile([P, S * PACK], BF16, align_bytes=64)
            grouped_of[(b, g)] = grouped
            for half in range(2):
                xt = psum_rot.tile([P, 2, 2 * P], F32, tag="rot")
                for u in range(2):
                    for jj in range(2):
                        nc.tensor.transpose(
                            xt[:, u, jj * P : (jj + 1) * P], words[:, 2 * half + jj, u, :], ident[:]
                        )
                columns = slice(HALF * PACK * half, HALF * PACK * (half + 1))
                nc.scalar.copy(
                    out=grouped[:, columns].bitcast(F32).rearrange("q (n u) -> q n u", u=2),
                    in_=xt[:].rearrange("q u n -> q n u"),
                )

        def quantise(b, g, first, count):
            if (b, g) not in mx_of:
                x_codes = mx_pool.tile([P, S], U32, align_bytes=256)
                x_planes = mx_pool.tile([P, S], U8, align_bytes=256)
                mx_of[(b, g)] = (x_codes, x_planes)
            x_codes, x_planes = mx_of[(b, g)]
            tokens = slice(P * first, P * (first + count))
            nc.vector.quantize_mx(
                out=x_codes[:, tokens].bitcast(FP8X4),
                scales=x_planes[:, tokens],
                in_=grouped_of[(b, g)][:, PACK * P * first : PACK * P * (first + count)],
            )

        def keep_warm(count):
            idle_ps = psum_rot.tile([P, P], F32, tag="rot")
            for i in range(count):
                nc.tensor.matmul(out=idle_ps[:], lhsT=zeros[:], rhs=zeros[:], start=True, stop=True)

        def turn_table(rows):
            table_ps = psum_rot.tile([P, S], BF16, tag="rot")
            for j in range(TOKEN_TILES):
                nc.tensor.transpose(table_ps[:, j * P : (j + 1) * P], rows[:, j, :], ident_bf[:])
            return table_ps

        keep_warm(WARM_BEFORE_X)
        for g in range(PASSES):
            turn_pass(0, g)
        quantise(0, 0, 0, 2)
        quantise(0, 0, 2, 2)

        bias_ps = psum_rot.tile([P, len(ROW_HEADS) * D + H], F32, tag="rot")
        for i, h in enumerate(ROW_HEADS):
            nc.tensor.matmul(
                out=bias_ps[:, i * D : (i + 1) * D],
                lhsT=ident_bf[:, h : h + 1].to_broadcast([P, P]),
                rhs=bq_rows[:],
                start=True,
                stop=True,
            )
        nc.tensor.matmul(
            out=bias_ps[:, len(ROW_HEADS) * D :], lhsT=bq_rows[:], rhs=ident_bf[:, 0:H], start=True, stop=True
        )
        bias_sb = const.tile([P, len(ROW_HEADS) * D + H], F32)
        nc.vector.tensor_copy(out=bias_sb[:], in_=bias_ps[:])
        bias = bias_sb[:, len(ROW_HEADS) * D :]
        quantise(0, 1, 0, 2)
        quantise(0, 1, 2, 2)

        tables_t = const.tile([P, 2, S], BF16)
        cos_ps = turn_table(cos_rows)
        nc.scalar.copy(out=tables_t[:, 0, :], in_=cos_ps[:])
        sin_pairs = sin_rows[:].rearrange("p j (i e) -> p (j i) e", e=2)
        partner_pairs = partner_rows.rearrange("p j (i e) -> p (j i) e", e=2)
        nc.vector.tensor_copy(out=partner_pairs[:, :, 0:1], in_=sin_pairs[:, :, 1:2])
        nc.vector.tensor_scalar_mul(out=partner_pairs[:, :, 1:2], in0=sin_pairs[:, :, 0:1], scalar1=-1.0)

        def pairs(tile):
            return tile[:].rearrange("p (i e) -> p i e", e=2)

        acc_of = {}
        lifted_of = {}
        made_of = {}

        def row_units(n):
            return round_units(n)[: row_count(n)]

        def turned_units(n):
            return round_units(n)[row_count(n) : row_count(n) + turned_count(n)]

        def column_units(n):
            return round_units(n)[row_count(n) + turned_count(n) :]

        def open_banks(n):
            for unit in round_units(n):
                acc = psum_acc.tile([P, S], F32, tag="acc")
                acc_of[unit] = acc

        def multiply_rows(unit):
            b, h = unit
            for j in range(TOKEN_TILES):
                columns = slice(j * P, (j + 1) * P)
                for g in range(PASSES):
                    x_codes, x_planes = mx_of[(b, g)]
                    nc.tensor.matmul_mx(
                        out=acc_of[unit][:, columns],
                        lhsT=x_codes[:, columns].bitcast(FP8X4),
                        lhsT_scale=x_planes[:, columns],
                        rhs=w_words[:, g, 2 * D * h : 2 * D * (h + 1)].bitcast(FP4X4),
                        rhs_scale=w_planes[:, g, D * h : D * (h + 1)],
                        start=(g == 0),
                        stop=(g == PASSES - 1),
                    )

        def row_products(unit):
            i = ROW_HEADS.index(unit[1])
            row_y = row_pool.tile([P, TOKEN_TILES, D], F32)
            nc.vector.tensor_tensor(
                out=row_y[:],
                in0=acc_of[unit][:].rearrange("p (j d) -> p j d", d=D),
                in1=bias_sb[:, i * D : (i + 1) * D].unsqueeze(1).to_broadcast([P, TOKEN_TILES, D]),
                op=ADD,
            )
            row_own = row_pool.tile([P, TOKEN_TILES * D], F32)
            nc.gpsimd.tensor_tensor(
                out=row_own[:].rearrange("p (j d) -> p j d", d=D), in0=row_y[:], in1=cos_rows, op=MULT
            )
            row_other = row_pool.tile([P, TOKEN_TILES * D], F32)
            nc.gpsimd.tensor_tensor(
                out=row_other[:].rearrange("p (j d) -> p j d", d=D), in0=row_y[:], in1=partner_rows, op=MULT
            )
            row_sum = row_pool.tile([P, TOKEN_TILES * D], F32)
            nc.gpsimd.tensor_tensor(
                out=pairs(row_sum), in0=pairs(row_own), in1=pairs(row_other)[:, :, ::-1], op=ADD
            )
            made_of[unit] = row_sum

        def finish_rows(unit, on_vector):
            b, h = unit
            res = res_pool.tile([P, TOKEN_TILES * D], F32)
            if on_vector:
                nc.vector.tensor_scalar_max(out=res[:], in0=made_of[unit][:], scalar1=0.0)
            else:
                nc.scalar.activation(out=res[:], in_=made_of[unit][:], func=RELU)
            nc.sync.dma_start(out=out[b, h].rearrange("(p j) d -> p (j d)", j=TOKEN_TILES), in_=res[:])

        def multiply_pass(unit, g):
            b, h = unit
            x_codes, x_planes = mx_of[(b, g)]
            nc.tensor.matmul_mx(
                out=acc_of[unit][:],
                lhsT=w_words[:, g, 2 * D * h : 2 * D * (h + 1)].bitcast(FP4X4),
                lhsT_scale=w_planes[:, g, D * h : D * (h + 1)],
                rhs=x_codes[:].bitcast(FP8X4),
                rhs_scale=x_planes[:],
                start=(g == 0),
                stop=(g == PASSES - 1),
            )

        def round_units(n):
            return [(unit // H, unit % H) for unit in range(GROUP * n, GROUP * (n + 1))]

        open_banks(0)
        for unit in column_units(0):
            multiply_pass(unit, 0)

        def products(unit):
            b, h = unit
            both = prod_pool.tile([P, 2, S], F32)
            nc.vector.scalar_tensor_tensor(
                out=both[:],
                in0=acc_of[unit][:].unsqueeze(1).to_broadcast([P, 2, S]),
                scalar=bias[:, h : h + 1],
                in1=tables_t[:],
                op0=ADD,
                op1=MULT,
            )
            made_of[unit] = (both[:, 0, :], both[:, 1, :])

        def lift(unit):
            y_sb = lift_pool.tile([P, S], F32)
            nc.scalar.activation(out=y_sb[:], in_=acc_of[unit][:], func=IDENTITY, bias=bias[:, unit[1] : unit[1] + 1])
            lifted_of[unit] = y_sb

        def turn_lifted(unit):
            rot = psum_rot.tile([P, TOKEN_TILES, D], F32, tag="rot")
            for j in range(TOKEN_TILES):
                nc.tensor.transpose(rot[:, j, :], lifted_of[unit][:, j * P : (j + 1) * P], ident[:])
            lifted_of[unit] = rot

        def turned_products(unit):
            both = row_pool.tile([P, 2, TOKEN_TILES * D], F32)
            nc.vector.tensor_tensor(
                out=both[:],
                in0=lifted_of[unit][:].rearrange("p j d -> p (j d)").unsqueeze(1).to_broadcast([P, 2, TOKEN_TILES * D]),
                in1=tables_rows[:].rearrange("p t j d -> p t (j d)"),
                op=MULT,
            )
            turned_sum = row_pool.tile([P, TOKEN_TILES * D], F32)
            own_pairs = both[:, 0, :].rearrange("p (i e) -> p i e", e=2)
            other_pairs = both[:, 1, :].rearrange("p (i e) -> p i e", e=2)
            nc.gpsimd.tensor_tensor(out=pairs(turned_sum), in0=own_pairs, in1=other_pairs[:, :, ::-1], op=ADD)
            made_of[unit] = turned_sum

        def turn_back(rot, unit, rows):
            own, other = made_of[unit]
            for i, j in enumerate(rows):
                tokens = slice(j * P, (j + 1) * P)
                nc.tensor.matmul(
                    out=rot[:, i, :], lhsT=own[:, tokens], rhs=ident[:], is_transpose=True, start=True, stop=False
                )
                nc.tensor.matmul(
                    out=rot[:, i, :], lhsT=other[:, tokens], rhs=pair_swap[:], is_transpose=True, start=False, stop=True
                )

        def finish(unit):
            b, h = unit
            rot = psum_rot.tile([P, TOKEN_TILES, D], F32, tag="rot")
            turn_back(rot, unit, range(TOKEN_TILES))
            res = res_pool.tile([P, TOKEN_TILES * D], F32)
            nc.scalar.activation(out=res[:], in_=rot[:].rearrange("p j d -> p (j d)"), func=RELU)
            nc.sync.dma_start(out=out[b, h].rearrange("(p j) d -> p (j d)", j=TOKEN_TILES), in_=res[:])

        def finish_last(unit):
            b, h = unit
            for part in range(2):
                rows = range(2 * part, 2 * part + 2)
                rot_half = psum_rot.tile([P, 2, D], F32, tag="rot")
                turn_back(rot_half, unit, rows)
                res_half = res_pool.tile([P, 2 * D], F32)
                source = rot_half[:].rearrange("p j d -> p (j d)")
                if part == 0:
                    nc.scalar.activation(out=res_half[:], in_=source, func=RELU)
                else:
                    nc.vector.tensor_scalar_max(out=res_half[:], in0=source, scalar1=0.0)
                nc.sync.dma_start(
                    out=out[b, h].rearrange("(p j) d -> p j d", j=TOKEN_TILES)[:, 2 * part : 2 * part + 2, :],
                    in_=res_half[:].rearrange("p (j d) -> p j d", d=D),
                )

        for n in range(ROUNDS + 1):
            turning = passes_of_round(n)
            for b, g in turning:
                if n > 0 or g == 0:
                    sort_pass(b, g)
            if n >= 1:
                for unit in turned_units(n - 1):
                    turned_products(unit)
                for b, g in passes_of_round(n - 1):
                    quantise(b, g, 0, TOKEN_TILES)
            if n < ROUNDS:
                if n > 0:
                    open_banks(n)
                for unit in row_units(n):
                    multiply_rows(unit)
                    row_products(unit)
                if n == 0:
                    partner_ps = turn_table(partner_rows)
                    nc.scalar.copy(out=tables_t[:, 1, :], in_=partner_ps[:])
                    sort_pass(1, 1)
                for unit in turned_units(n):
                    for g in range(PASSES):
                        multiply_pass(unit, g)
                    lift(unit)
                for unit in column_units(n):
                    for g in range(PASSES):
                        if n > 0 or g > 0:
                            multiply_pass(unit, g)
                    products(unit)
            if n >= 1:
                before = column_units(n - 1)
                if n < ROUNDS:
                    for unit in before:
                        finish(unit)
                else:
                    for unit in before[:-1]:
                        finish(unit)
                    for unit in row_units(n - 2):
                        finish_rows(unit, on_vector=True)
                    finish_last(before[-1])
            for b, g in turning:
                turn_pass(b, g)
            for unit in turned_units(n):
                turn_lifted(unit)
            if 1 <= n < ROUNDS - 1:
                for unit in row_units(n - 1) + turned_units(n - 1):
                    finish_rows(unit, on_vector=False)
